import numpy as np
import ml_dtypes


def mxq(x, axis, fmt="e4m3"):
    dtype, down = {"e4m3": (ml_dtypes.float8_e4m3fn, 7), "e5m2": (ml_dtypes.float8_e5m2, 14)}[fmt]
    v = np.moveaxis(np.asarray(x, np.float32).astype(ml_dtypes.bfloat16).astype(np.float64), axis, -1)
    blocks = v.reshape(v.shape[:-1] + (-1, 32))
    amax = np.abs(blocks).max(-1, keepdims=True)
    byte = np.maximum(np.where(amax > 0, np.frexp(amax)[1] - 1 + 127, 0) - down, 1)
    scale = np.exp2(byte - 127.0)
    codes = (blocks / scale).astype(np.float32).astype(dtype).astype(np.float64)
    return np.moveaxis((codes * scale).reshape(v.shape), -1, axis)


BF16 = ml_dtypes.bfloat16


def bf(x):
    return np.asarray(x, np.float32).astype(BF16)


def f64(x):
    return np.asarray(x).astype(np.float64)


B, D_IN, H1, H2, H3, C = 8192, 2048, 1024, 512, 1024, 1024
BN_EPS = 1e-5


def binarize(w):
    return np.where(w >= 0, 1.0, -1.0)


def bn_relu(z, gamma, beta):
    m = z.mean(axis=0)
    v = z.var(axis=0)
    return np.maximum((z - m) * (1.0 / np.sqrt(v + BN_EPS)) * gamma + beta, 0.0)


def setup_inputs():
    c = 4.0 * np.exp2(-12.0 * np.random.random(H1))
    mu = 0.5 * np.random.standard_normal(H1)
    return {"z0": bf((np.random.standard_normal((B, H1)) + mu) * c),
            "g0": bf(0.25 * (1.0 + 0.1 * np.random.standard_normal(H1))),
            "beta0": bf(0.1 * np.random.standard_normal(H1)),
            "Wb1": bf(np.random.standard_normal((H2, H1)) / np.sqrt(H1)),
            "bb1": bf(np.random.standard_normal(H2))}


def reference(z0, g0, beta0, Wb1, bb1):
    h = bn_relu(f64(z0), f64(g0), f64(beta0))
    ws = binarize(f64(Wb1))
    return (mxq(h, 1, "e4m3") @ mxq(ws, 1, "e4m3").T) + f64(bb1)

@@ -1,0 +1,158 @@
+import concourse.mybir as mybir
+from concourse.masks import make_identity
+
+FP32 = mybir.dt.float32
+BF16 = mybir.dt.bfloat16
+U32 = mybir.dt.uint32
+U8 = mybir.dt.uint8
+FP8X4 = mybir.dt.float8_e4m3fn_x4
+ALU = mybir.AluOpType
+ACT = mybir.ActivationFunctionType
+
+P = 128
+PACK = 4
+BATCH, FEATS, OUTS = 8192, 1024, 512
+BN_EPS = 1e-5
+FLOPS = 2 * BATCH * FEATS * OUTS
+
+K_BLOCKS = FEATS // P
+PASSES = K_BLOCKS // PACK
+ROW_TILES = 4
+CHUNK = ROW_TILES * P
+N_CHUNKS = BATCH // CHUNK
+WIDE = 4 * CHUNK
+STATS = 6
+
+
+def tile_binarymlp_pa_t_kernel(tc, z0, g0, beta0, Wb1, bb1, out):
+    nc = tc.nc
+    with tc.tile_pool(name="keep", bufs=1) as keep:
+        ident = keep.tile([P, P], BF16)
+        make_identity(nc, ident[:])
+        zT = keep.tile([P, K_BLOCKS, BATCH], BF16)
+        w_codes = keep.tile([P, PASSES, OUTS], U32, align_bytes=64)
+        w_scales = keep.tile([P, PASSES, OUTS], U8, align_bytes=64)
+        bias_all = keep.tile([P, OUTS], FP32)
+        gain = keep.tile([P, K_BLOCKS], FP32)
+        shift = keep.tile([P, K_BLOCKS], FP32)
+
+        one = keep.tile([P, 1], FP32)
+        nc.vector.memset(one[:], 1.0)
+        warm = keep.tile([P, 1], FP32)
+        nc.scalar.sqrt(out=warm[:], in_=one[:])
+
+        with tc.tile_pool(name="setup", bufs=1) as setup, tc.tile_pool(name="load", bufs=4) as load, tc.psum_pool(
+            name="setup_ps", bufs=2
+        ) as setup_ps, tc.psum_pool(name="turn_ps", bufs=4) as turn_ps:
+            vec_rows = setup.tile([P, P], BF16)
+            nc.vector.memset(vec_rows[:], 0.0)
+            nc.scalar.dma_start(out=vec_rows[0:K_BLOCKS, :], in_=g0.rearrange("(c p) -> c p", p=P))
+            nc.scalar.dma_start(out=vec_rows[K_BLOCKS : 2 * K_BLOCKS, :], in_=beta0.rearrange("(c p) -> c p", p=P))
+            vec_ps = setup_ps.tile([P, P], BF16, tag="setup")
+            nc.tensor.transpose(vec_ps[:], vec_rows[:], ident[:])
+            vec_cols = setup.tile([P, 2 * K_BLOCKS], FP32)
+            nc.vector.tensor_copy(out=vec_cols[:], in_=vec_ps[:, 0 : 2 * K_BLOCKS])
+
+            bias_row = setup.tile([P, OUTS], BF16)
+            nc.vector.memset(bias_row[:], 0.0)
+            nc.scalar.dma_start(out=bias_row[0:1, :], in_=bb1.rearrange("(o n) -> o n", o=1))
+            ones = setup.tile([P, P], BF16)
+            nc.vector.memset(ones[:], 1.0)
+            bias_ps = setup_ps.tile([P, OUTS], FP32, tag="setup")
+            nc.tensor.matmul(out=bias_ps[:], lhsT=ones[:], rhs=bias_row[:], start=True, stop=True)
+            nc.vector.tensor_copy(out=bias_all[:], in_=bias_ps[:])
+
+            w_rows = setup.tile([P, OUTS // P, FEATS], BF16)
+            nc.scalar.dma_start(out=w_rows[:], in_=Wb1.rearrange("(a p) k -> p a k", p=P))
+            w_two = setup.tile([P, OUTS // P, FEATS], BF16)
+            nc.vector.tensor_scalar(out=w_two[:], in0=w_rows[:], scalar1=0.0, scalar2=2.0, op0=ALU.is_ge, op1=ALU.mult)
+            w_grouped = setup.tile([P, PASSES, OUTS, PACK], BF16, align_bytes=64)
+            for g in range(PASSES):
+                for a in range(OUTS // P):
+                    w_ps = setup_ps.tile([P, PACK, P], BF16, tag="setup")
+                    for t in range(PACK):
+                        c = PACK * g + t
+                        nc.tensor.transpose(w_ps[:, t, :], w_two[:, a, c * P : (c + 1) * P], ident[:])
+                    nc.vector.tensor_scalar_add(
+                        out=w_grouped[:, g, a * P : (a + 1) * P, :],
+                        in0=w_ps[:].rearrange("p t n -> p n t"),
+                        scalar1=-1.0,
+                    )
+                nc.vector.quantize_mx(
+                    out=w_codes[:, g, :].bitcast(FP8X4),
+                    scales=w_scales[:, g, :],
+                    in_=w_grouped[:, g, :, :].rearrange("p n t -> p (n t)"),
+                )
+
+            stats = setup.tile([P, K_BLOCKS, N_CHUNKS, STATS], FP32)
+            for i in range(N_CHUNKS):
+                cols = slice(i * CHUNK, (i + 1) * CHUNK)
+                z_rows = load.tile([P, ROW_TILES, FEATS], BF16)
+                nc.sync.dma_start(out=z_rows[:], in_=z0[cols, :].rearrange("(p j) f -> p j f", j=ROW_TILES))
+                for c in range(K_BLOCKS):
+                    turned = turn_ps.tile([P, ROW_TILES, P], BF16)
+                    for j in range(ROW_TILES):
+                        nc.tensor.transpose(turned[:, j, :], z_rows[:, j, c * P : (c + 1) * P], ident[:])
+                    nc.scalar.copy(out=zT[:, c, cols], in_=turned[:].rearrange("p j r -> p (j r)"))
+                    nc.vector.bn_stats(out=stats[:, c, i, :], in_=zT[:, c, cols])
+
+            mean_var = setup.tile([P, K_BLOCKS, 2], FP32)
+            for c in range(K_BLOCKS):
+                nc.vector.bn_aggr(out=mean_var[:, c, :], in_=stats[:, c, :, :].rearrange("p i s -> p (i s)"))
+            var_eps = setup.tile([P, K_BLOCKS], FP32)
+            nc.vector.tensor_scalar_add(out=var_eps[:], in0=mean_var[:, :, 1], scalar1=BN_EPS)
+            std = setup.tile([P, K_BLOCKS], FP32)
+            nc.scalar.sqrt(out=std[:], in_=var_eps[:])
+            rstd = setup.tile([P, K_BLOCKS], FP32)
+            nc.vector.reciprocal(out=rstd[:], in_=std[:])
+            nc.vector.tensor_mul(out=gain[:], in0=vec_cols[:, 0:K_BLOCKS], in1=rstd[:])
+            mean_gain = setup.tile([P, K_BLOCKS], FP32)
+            nc.vector.tensor_mul(out=mean_gain[:], in0=mean_var[:, :, 0], in1=gain[:])
+            nc.vector.tensor_sub(out=shift[:], in0=vec_cols[:, K_BLOCKS : 2 * K_BLOCKS], in1=mean_gain[:])
+
+        with tc.tile_pool(name="group", bufs=4) as group, tc.tile_pool(name="mx", bufs=3) as mx, tc.tile_pool(
+            name="res", bufs=3
+        ) as res, tc.psum_pool(name="acc_ps", bufs=6) as acc_ps:
+            for i in range(N_CHUNKS):
+                if (i * CHUNK) % WIDE == 0:
+                    wide = slice(i * CHUNK, i * CHUNK + WIDE)
+                    for c in range(K_BLOCKS):
+                        nc.vector.tensor_scalar(
+                            out=zT[:, c, wide],
+                            in0=zT[:, c, wide],
+                            scalar1=gain[:, c : c + 1],
+                            scalar2=shift[:, c : c + 1],
+                            op0=ALU.mult,
+                            op1=ALU.add,
+                        )
+                cols = slice(i * CHUNK, (i + 1) * CHUNK)
+                h_codes = mx.tile([P, PASSES, CHUNK], U32, align_bytes=64)
+                h_scales = mx.tile([P, PASSES, CHUNK], U8, align_bytes=64)
+                for g in range(PASSES):
+                    grouped = group.tile([P, CHUNK, PACK], BF16, align_bytes=64)
+                    nc.scalar.activation(
+                        out=grouped[:].rearrange("p (q i) t -> p q t i", i=4),
+                        in_=zT[:, PACK * g : PACK * (g + 1), cols].rearrange("p t (q i) -> p q t i", i=4),
+                        func=ACT.Relu,
+                    )
+                    nc.vector.quantize_mx(
+                        out=h_codes[:, g, :].bitcast(FP8X4),
+                        scales=h_scales[:, g, :],
+                        in_=grouped[:].rearrange("p w t -> p (w t)"),
+                    )
+                result = res.tile([P, ROW_TILES, OUTS], FP32)
+                for j in range(ROW_TILES):
+                    rows = slice(j * P, (j + 1) * P)
+                    acc = acc_ps.tile([P, OUTS], FP32)
+                    for g in range(PASSES):
+                        nc.tensor.matmul_mx(
+                            out=acc[:],
+                            lhsT=h_codes[:, g, rows].bitcast(FP8X4),
+                            lhsT_scale=h_scales[:, g, rows],
+                            rhs=w_codes[:, g, :].bitcast(FP8X4),
+                            rhs_scale=w_scales[:, g, :],
+                            start=(g == 0),
+                            stop=(g == PASSES - 1),
+                        )
+                    nc.vector.tensor_tensor(out=result[:, j, :], in0=acc[:], in1=bias_all[:], op=ALU.add)
+                nc.sync.dma_start(out=out[cols, :].rearrange("(p j) n -> p j n", j=ROW_TILES), in_=result[:])

@@ -8,6 +8,7 @@ U8 = mybir.dt.uint8
 FP8X4 = mybir.dt.float8_e4m3fn_x4
 ALU = mybir.AluOpType
 ACT = mybir.ActivationFunctionType
+AXIS = mybir.AxisListType
 
 P = 128
 PACK = 4
@@ -17,16 +18,18 @@ FLOPS = 2 * BATCH * FEATS * OUTS
 
 K_BLOCKS = FEATS // P
 PASSES = K_BLOCKS // PACK
+OUT_TILES = OUTS // P
 ROW_TILES = 4
 CHUNK = ROW_TILES * P
 N_CHUNKS = BATCH // CHUNK
-WIDE = 4 * CHUNK
-STATS = 6
+N_PAIRS = N_CHUNKS // 2
+TRIPLES = 2 * N_PAIRS + 1
+SUMMED = N_PAIRS * CHUNK
 
 
 def tile_binarymlp_pa_t_kernel(tc, z0, g0, beta0, Wb1, bb1, out):
     nc = tc.nc
-    with tc.tile_pool(name="keep", bufs=1) as keep:
+    with tc.manual_schedule(), tc.tile_pool(name="keep", bufs=1) as keep:
         ident = keep.tile([P, P], BF16)
         make_identity(nc, ident[:])
         zT = keep.tile([P, K_BLOCKS, BATCH], BF16)
@@ -41,68 +44,124 @@ def tile_binarymlp_pa_t_kernel(tc, z0, g0, beta0, Wb1, bb1, out):
         warm = keep.tile([P, 1], FP32)
         nc.scalar.sqrt(out=warm[:], in_=one[:])
 
-        with tc.tile_pool(name="setup", bufs=1) as setup, tc.tile_pool(name="load", bufs=4) as load, tc.psum_pool(
-            name="setup_ps", bufs=2
-        ) as setup_ps, tc.psum_pool(name="turn_ps", bufs=4) as turn_ps:
+        with tc.tile_pool(name="setup", bufs=1) as setup, tc.tile_pool(name="load", bufs=2) as load, tc.tile_pool(
+            name="waste", bufs=4
+        ) as waste, tc.psum_pool(name="setup_ps", bufs=2) as setup_ps, tc.psum_pool(name="turn_ps", bufs=3) as turn_ps:
             vec_rows = setup.tile([P, P], BF16)
             nc.vector.memset(vec_rows[:], 0.0)
-            nc.scalar.dma_start(out=vec_rows[0:K_BLOCKS, :], in_=g0.rearrange("(c p) -> c p", p=P))
-            nc.scalar.dma_start(out=vec_rows[K_BLOCKS : 2 * K_BLOCKS, :], in_=beta0.rearrange("(c p) -> c p", p=P))
+            nc.sync.dma_start(out=vec_rows[0:K_BLOCKS, :], in_=g0.rearrange("(c p) -> c p", p=P))
+            nc.sync.dma_start(out=vec_rows[K_BLOCKS : 2 * K_BLOCKS, :], in_=beta0.rearrange("(c p) -> c p", p=P))
+            bias_row = setup.tile([P, OUTS], BF16)
+            nc.vector.memset(bias_row[:], 0.0)
+            nc.sync.dma_start(out=bias_row[0:1, :], in_=bb1.rearrange("(o n) -> o n", o=1))
+            ones = setup.tile([P, P], BF16)
+            nc.vector.memset(ones[:], 1.0)
+
             vec_ps = setup_ps.tile([P, P], BF16, tag="setup")
             nc.tensor.transpose(vec_ps[:], vec_rows[:], ident[:])
             vec_cols = setup.tile([P, 2 * K_BLOCKS], FP32)
             nc.vector.tensor_copy(out=vec_cols[:], in_=vec_ps[:, 0 : 2 * K_BLOCKS])
-
-            bias_row = setup.tile([P, OUTS], BF16)
-            nc.vector.memset(bias_row[:], 0.0)
-            nc.scalar.dma_start(out=bias_row[0:1, :], in_=bb1.rearrange("(o n) -> o n", o=1))
-            ones = setup.tile([P, P], BF16)
-            nc.vector.memset(ones[:], 1.0)
             bias_ps = setup_ps.tile([P, OUTS], FP32, tag="setup")
             nc.tensor.matmul(out=bias_ps[:], lhsT=ones[:], rhs=bias_row[:], start=True, stop=True)
             nc.vector.tensor_copy(out=bias_all[:], in_=bias_ps[:])
 
-            w_rows = setup.tile([P, OUTS // P, FEATS], BF16)
-            nc.scalar.dma_start(out=w_rows[:], in_=Wb1.rearrange("(a p) k -> p a k", p=P))
-            w_two = setup.tile([P, OUTS // P, FEATS], BF16)
-            nc.vector.tensor_scalar(out=w_two[:], in0=w_rows[:], scalar1=0.0, scalar2=2.0, op0=ALU.is_ge, op1=ALU.mult)
+            stats = setup.tile([P, K_BLOCKS, TRIPLES, 3], FP32)
+            nc.vector.memset(stats[:, :, TRIPLES - 1, 0:1], float(SUMMED))
+            sums = setup.tile([P, K_BLOCKS, N_PAIRS], FP32)
+            squares = setup.tile([P, K_BLOCKS, N_PAIRS], FP32)
+            neg_pivot = setup.tile([P, K_BLOCKS], FP32)
+            w_rows = setup.tile([P, OUT_TILES, FEATS], BF16)
+            w_two = setup.tile([P, OUT_TILES, FEATS], BF16)
+            for pair in range(N_PAIRS):
+                cols_a = slice((2 * pair) * CHUNK, (2 * pair + 1) * CHUNK)
+                cols_b = slice((2 * pair + 1) * CHUNK, (2 * pair + 2) * CHUNK)
+                rows_a = load.tile([P, ROW_TILES, FEATS], BF16)
+                nc.sync.dma_start(out=rows_a[:], in_=z0[cols_a, :].rearrange("(p j) f -> p j f", j=ROW_TILES))
+                rows_b = load.tile([P, ROW_TILES, FEATS], BF16)
+                nc.sync.dma_start(out=rows_b[:], in_=z0[cols_b, :].rearrange("(p j) f -> p j f", j=ROW_TILES))
+                if pair == 1:
+                    nc.sync.dma_start(out=w_rows[:], in_=Wb1.rearrange("(a p) k -> p a k", p=P))
+                    nc.gpsimd.tensor_scalar(
+                        out=w_two[:], in0=w_rows[:], scalar1=0.0, scalar2=2.0, op0=ALU.is_ge, op1=ALU.mult
+                    )
+                for c in range(K_BLOCKS):
+                    feats = slice(c * P, (c + 1) * P)
+                    turned_a = turn_ps.tile([P, ROW_TILES, P], BF16)
+                    for j in range(ROW_TILES):
+                        nc.tensor.transpose(turned_a[:, j, :], rows_a[:, j, feats], ident[:])
+                    turned_b = turn_ps.tile([P, ROW_TILES, P], BF16)
+                    for j in range(ROW_TILES):
+                        nc.tensor.transpose(turned_b[:, j, :], rows_b[:, j, feats], ident[:])
+                    nc.vector.tensor_scalar(
+                        out=zT[:, c, cols_a],
+                        in0=turned_a[:].rearrange("p j r -> p (j r)"),
+                        scalar1=1.0,
+                        scalar2=None,
+                        op0=ALU.mult,
+                        op1=ALU.add,
+                        accum_out=sums[:, c, pair : pair + 1],
+                    )
+                    nc.scalar.copy(out=zT[:, c, cols_b], in_=turned_b[:].rearrange("p j r -> p (j r)"))
+                    if pair == 0:
+                        nc.vector.tensor_scalar_mul(
+                            out=neg_pivot[:, c : c + 1], in0=sums[:, c, 0:1], scalar1=-1.0 / CHUNK
+                        )
+                    unread = waste.tile([P, CHUNK], BF16)
+                    nc.scalar.activation(
+                        out=unread[:],
+                        in_=zT[:, c, cols_a],
+                        func=ACT.Square,
+                        bias=neg_pivot[:, c : c + 1],
+                        scale=1.0,
+                        accum_out=squares[:, c, pair : pair + 1],
+                    )
+                    nc.vector.bn_stats(
+                        out=stats[:, c, 2 * pair : 2 * pair + 2, :].rearrange("p a s -> p (a s)"), in_=zT[:, c, cols_b]
+                    )
+
             w_grouped = setup.tile([P, PASSES, OUTS, PACK], BF16, align_bytes=64)
-            for g in range(PASSES):
-                for a in range(OUTS // P):
+
+            def turn_weights(g):
+                for a in range(OUT_TILES):
                     w_ps = setup_ps.tile([P, PACK, P], BF16, tag="setup")
                     for t in range(PACK):
                         c = PACK * g + t
                         nc.tensor.transpose(w_ps[:, t, :], w_two[:, a, c * P : (c + 1) * P], ident[:])
-                    nc.vector.tensor_scalar_add(
+                    nc.scalar.activation(
                         out=w_grouped[:, g, a * P : (a + 1) * P, :],
-                        in0=w_ps[:].rearrange("p t n -> p n t"),
-                        scalar1=-1.0,
+                        in_=w_ps[:].rearrange("p t n -> p n t"),
+                        func=ACT.Copy,
+                        bias=-1.0,
+                        scale=1.0,
                     )
-                nc.vector.quantize_mx(
-                    out=w_codes[:, g, :].bitcast(FP8X4),
-                    scales=w_scales[:, g, :],
-                    in_=w_grouped[:, g, :, :].rearrange("p n t -> p (n t)"),
-                )
 
-            stats = setup.tile([P, K_BLOCKS, N_CHUNKS, STATS], FP32)
-            for i in range(N_CHUNKS):
-                cols = slice(i * CHUNK, (i + 1) * CHUNK)
-                z_rows = load.tile([P, ROW_TILES, FEATS], BF16)
-                nc.sync.dma_start(out=z_rows[:], in_=z0[cols, :].rearrange("(p j) f -> p j f", j=ROW_TILES))
-                for c in range(K_BLOCKS):
-                    turned = turn_ps.tile([P, ROW_TILES, P], BF16)
-                    for j in range(ROW_TILES):
-                        nc.tensor.transpose(turned[:, j, :], z_rows[:, j, c * P : (c + 1) * P], ident[:])
-                    nc.scalar.copy(out=zT[:, c, cols], in_=turned[:].rearrange("p j r -> p (j r)"))
-                    nc.vector.bn_stats(out=stats[:, c, i, :], in_=zT[:, c, cols])
-
+            turn_weights(0)
+            sum_a = setup.tile([P, K_BLOCKS], FP32)
+            nc.vector.tensor_reduce(out=sum_a[:], in_=sums[:], axis=AXIS.X, op=ALU.add)
+            square_a = setup.tile([P, K_BLOCKS], FP32)
+            nc.vector.tensor_reduce(out=square_a[:], in_=squares[:], axis=AXIS.X, op=ALU.add)
+            mean_a = stats[:, :, TRIPLES - 1, 1]
+            nc.vector.tensor_scalar_mul(out=mean_a, in0=sum_a[:], scalar1=1.0 / SUMMED)
+            off = setup.tile([P, K_BLOCKS], FP32)
+            nc.vector.tensor_add(out=off[:], in0=mean_a, in1=neg_pivot[:])
+            off_sq = setup.tile([P, K_BLOCKS], FP32)
+            nc.vector.tensor_mul(out=off_sq[:], in0=off[:], in1=off[:])
+            nc.vector.scalar_tensor_tensor(
+                out=stats[:, :, TRIPLES - 1, 2],
+                in0=off_sq[:],
+                scalar=-float(SUMMED),
+                in1=square_a[:],
+                op0=ALU.mult,
+                op1=ALU.add,
+            )
             mean_var = setup.tile([P, K_BLOCKS, 2], FP32)
             for c in range(K_BLOCKS):
-                nc.vector.bn_aggr(out=mean_var[:, c, :], in_=stats[:, c, :, :].rearrange("p i s -> p (i s)"))
+                nc.vector.bn_aggr(out=mean_var[:, c, :], in_=stats[:, c, :, :].rearrange("p a s -> p (a s)"))
             var_eps = setup.tile([P, K_BLOCKS], FP32)
             nc.vector.tensor_scalar_add(out=var_eps[:], in0=mean_var[:, :, 1], scalar1=BN_EPS)
             std = setup.tile([P, K_BLOCKS], FP32)
             nc.scalar.sqrt(out=std[:], in_=var_eps[:])
+            turn_weights(1)
             rstd = setup.tile([P, K_BLOCKS], FP32)
             nc.vector.reciprocal(out=rstd[:], in_=std[:])
             nc.vector.tensor_mul(out=gain[:], in0=vec_cols[:, 0:K_BLOCKS], in1=rstd[:])
@@ -110,49 +169,83 @@ def tile_binarymlp_pa_t_kernel(tc, z0, g0, beta0, Wb1, bb1, out):
             nc.vector.tensor_mul(out=mean_gain[:], in0=mean_var[:, :, 0], in1=gain[:])
             nc.vector.tensor_sub(out=shift[:], in0=vec_cols[:, K_BLOCKS : 2 * K_BLOCKS], in1=mean_gain[:])
 
-        with tc.tile_pool(name="group", bufs=4) as group, tc.tile_pool(name="mx", bufs=3) as mx, tc.tile_pool(
-            name="res", bufs=3
-        ) as res, tc.psum_pool(name="acc_ps", bufs=6) as acc_ps:
-            for i in range(N_CHUNKS):
-                if (i * CHUNK) % WIDE == 0:
-                    wide = slice(i * CHUNK, i * CHUNK + WIDE)
-                    for c in range(K_BLOCKS):
-                        nc.vector.tensor_scalar(
-                            out=zT[:, c, wide],
-                            in0=zT[:, c, wide],
-                            scalar1=gain[:, c : c + 1],
-                            scalar2=shift[:, c : c + 1],
-                            op0=ALU.mult,
-                            op1=ALU.add,
-                        )
+            def normalise(i):
                 cols = slice(i * CHUNK, (i + 1) * CHUNK)
-                h_codes = mx.tile([P, PASSES, CHUNK], U32, align_bytes=64)
-                h_scales = mx.tile([P, PASSES, CHUNK], U8, align_bytes=64)
+                for c in range(K_BLOCKS):
+                    nc.vector.tensor_scalar(
+                        out=zT[:, c, cols],
+                        in0=zT[:, c, cols],
+                        scalar1=gain[:, c : c + 1],
+                        scalar2=shift[:, c : c + 1],
+                        op0=ALU.mult,
+                        op1=ALU.add,
+                    )
+
+            normalise(0)
+            normalise(1)
+            nc.vector.quantize_mx(
+                out=w_codes[:].rearrange("p g n -> p (g n)").bitcast(FP8X4),
+                scales=w_scales[:].rearrange("p g n -> p (g n)"),
+                in_=w_grouped[:].rearrange("p g n t -> p (g n t)"),
+            )
+
+        with tc.tile_pool(name="group", bufs=3) as group, tc.tile_pool(name="mx", bufs=3) as mx, tc.tile_pool(
+            name="res", bufs=3
+        ) as res, tc.psum_pool(name="acc_ps", bufs=8) as acc_ps:
+            grouped = {}
+            h_codes = {}
+            h_scales = {}
+
+            def regroup(i):
+                cols = slice(i * CHUNK, (i + 1) * CHUNK)
+                grouped[i] = group.tile([P, PASSES, CHUNK, PACK], BF16, align_bytes=64, name="grouped")
                 for g in range(PASSES):
-                    grouped = group.tile([P, CHUNK, PACK], BF16, align_bytes=64)
                     nc.scalar.activation(
-                        out=grouped[:].rearrange("p (q i) t -> p q t i", i=4),
+                        out=grouped[i][:, g, :, :].rearrange("p (q i) t -> p q t i", i=4),
                         in_=zT[:, PACK * g : PACK * (g + 1), cols].rearrange("p t (q i) -> p q t i", i=4),
                         func=ACT.Relu,
                     )
-                    nc.vector.quantize_mx(
-                        out=h_codes[:, g, :].bitcast(FP8X4),
-                        scales=h_scales[:, g, :],
-                        in_=grouped[:].rearrange("p w t -> p (w t)"),
-                    )
-                result = res.tile([P, ROW_TILES, OUTS], FP32)
+
+            def quantise(i):
+                h_codes[i] = mx.tile([P, PASSES, CHUNK], U32, align_bytes=64, name="h_codes")
+                h_scales[i] = mx.tile([P, PASSES, CHUNK], U8, align_bytes=64, name="h_scales")
+                nc.vector.quantize_mx(
+                    out=h_codes[i][:].rearrange("p g w -> p (g w)").bitcast(FP8X4),
+                    scales=h_scales[i][:].rearrange("p g w -> p (g w)"),
+                    in_=grouped[i][:].rearrange("p g w t -> p (g w t)"),
+                )
+
+            def multiply(i):
+                accs = []
                 for j in range(ROW_TILES):
                     rows = slice(j * P, (j + 1) * P)
                     acc = acc_ps.tile([P, OUTS], FP32)
                     for g in range(PASSES):
                         nc.tensor.matmul_mx(
                             out=acc[:],
-                            lhsT=h_codes[:, g, rows].bitcast(FP8X4),
-                            lhsT_scale=h_scales[:, g, rows],
+                            lhsT=h_codes[i][:, g, rows].bitcast(FP8X4),
+                            lhsT_scale=h_scales[i][:, g, rows],
                             rhs=w_codes[:, g, :].bitcast(FP8X4),
                             rhs_scale=w_scales[:, g, :],
                             start=(g == 0),
                             stop=(g == PASSES - 1),
                         )
-                    nc.vector.tensor_tensor(out=result[:, j, :], in0=acc[:], in1=bias_all[:], op=ALU.add)
+                    accs.append(acc)
+                return accs
+
+            def finish(i, accs):
+                cols = slice(i * CHUNK, (i + 1) * CHUNK)
+                result = res.tile([P, ROW_TILES, OUTS], FP32)
+                for j in range(ROW_TILES):
+                    nc.vector.tensor_tensor(out=result[:, j, :], in0=accs[j][:], in1=bias_all[:], op=ALU.add)
                 nc.sync.dma_start(out=out[cols, :].rearrange("(p j) n -> p j n", j=ROW_TILES), in_=result[:])
+
+            regroup(0)
+            for i in range(N_CHUNKS):
+                if i + 1 < N_CHUNKS:
+                    regroup(i + 1)
+                quantise(i)
+                accs = multiply(i)
+                if i + 2 < N_CHUNKS:
+                    normalise(i + 2)
+                finish(i, accs)

@@ -25,6 +25,10 @@ N_CHUNKS = BATCH // CHUNK
 N_PAIRS = N_CHUNKS // 2
 TRIPLES = 2 * N_PAIRS + 1
 SUMMED = N_PAIRS * CHUNK
+WIDE = 4 * CHUNK
+PIECES = K_BLOCKS * (BATCH // WIDE)
+PIECES_A_STEP = PIECES // N_CHUNKS
+PIECES_AHEAD = K_BLOCKS + PIECES_A_STEP
 
 
 def tile_binarymlp_pa_t_kernel(tc, z0, g0, beta0, Wb1, bb1, out):
@@ -44,9 +48,9 @@ def tile_binarymlp_pa_t_kernel(tc, z0, g0, beta0, Wb1, bb1, out):
         warm = keep.tile([P, 1], FP32)
         nc.scalar.sqrt(out=warm[:], in_=one[:])
 
-        with tc.tile_pool(name="setup", bufs=1) as setup, tc.tile_pool(name="load", bufs=2) as load, tc.tile_pool(
-            name="waste", bufs=4
-        ) as waste, tc.psum_pool(name="setup_ps", bufs=2) as setup_ps, tc.psum_pool(name="turn_ps", bufs=3) as turn_ps:
+        with tc.tile_pool(name="load", bufs=3) as load, tc.tile_pool(name="waste", bufs=4) as waste, tc.tile_pool(
+            name="setup", bufs=1
+        ) as setup, tc.psum_pool(name="turn_ps", bufs=3) as turn_ps, tc.psum_pool(name="setup_ps", bufs=2) as setup_ps:
             vec_rows = setup.tile([P, P], BF16)
             nc.vector.memset(vec_rows[:], 0.0)
             nc.sync.dma_start(out=vec_rows[0:K_BLOCKS, :], in_=g0.rearrange("(c p) -> c p", p=P))
@@ -72,52 +76,71 @@ def tile_binarymlp_pa_t_kernel(tc, z0, g0, beta0, Wb1, bb1, out):
             neg_pivot = setup.tile([P, K_BLOCKS], FP32)
             w_rows = setup.tile([P, OUT_TILES, FEATS], BF16)
             w_two = setup.tile([P, OUT_TILES, FEATS], BF16)
-            for pair in range(N_PAIRS):
-                cols_a = slice((2 * pair) * CHUNK, (2 * pair + 1) * CHUNK)
-                cols_b = slice((2 * pair + 1) * CHUNK, (2 * pair + 2) * CHUNK)
-                rows_a = load.tile([P, ROW_TILES, FEATS], BF16)
-                nc.sync.dma_start(out=rows_a[:], in_=z0[cols_a, :].rearrange("(p j) f -> p j f", j=ROW_TILES))
-                rows_b = load.tile([P, ROW_TILES, FEATS], BF16)
-                nc.sync.dma_start(out=rows_b[:], in_=z0[cols_b, :].rearrange("(p j) f -> p j f", j=ROW_TILES))
-                if pair == 1:
+            rows_a = {}
+            rows_b = {}
+
+            def columns(pair):
+                first = 2 * pair * CHUNK
+                return slice(first, first + CHUNK), slice(first + CHUNK, first + 2 * CHUNK)
+
+            def load_pair(pair):
+                cols_a, cols_b = columns(pair)
+                rows_a[pair] = load.tile([P, ROW_TILES, FEATS], BF16, name="rows_a")
+                nc.sync.dma_start(out=rows_a[pair][:], in_=z0[cols_a, :].rearrange("(p j) f -> p j f", j=ROW_TILES))
+                rows_b[pair] = load.tile([P, ROW_TILES, FEATS], BF16, name="rows_b")
+                nc.sync.dma_start(out=rows_b[pair][:], in_=z0[cols_b, :].rearrange("(p j) f -> p j f", j=ROW_TILES))
+
+            def turn(pair, c):
+                cols_a, cols_b = columns(pair)
+                feats = slice(c * P, (c + 1) * P)
+                turned_a = turn_ps.tile([P, ROW_TILES, P], BF16)
+                for j in range(ROW_TILES):
+                    nc.tensor.transpose(turned_a[:, j, :], rows_a[pair][:, j, feats], ident[:])
+                turned_b = turn_ps.tile([P, ROW_TILES, P], BF16)
+                for j in range(ROW_TILES):
+                    nc.tensor.transpose(turned_b[:, j, :], rows_b[pair][:, j, feats], ident[:])
+                nc.vector.tensor_scalar(
+                    out=zT[:, c, cols_a],
+                    in0=turned_a[:].rearrange("p j r -> p (j r)"),
+                    scalar1=1.0,
+                    scalar2=None,
+                    op0=ALU.mult,
+                    op1=ALU.add,
+                    accum_out=sums[:, c, pair : pair + 1],
+                )
+                nc.scalar.copy(out=zT[:, c, cols_b], in_=turned_b[:].rearrange("p j r -> p (j r)"))
+                if pair == 0:
+                    nc.vector.tensor_scalar_mul(out=neg_pivot[:, c : c + 1], in0=sums[:, c, 0:1], scalar1=-1.0 / CHUNK)
+
+            def measure(pair, c):
+                cols_a, cols_b = columns(pair)
+                unread = waste.tile([P, CHUNK], BF16)
+                nc.scalar.activation(
+                    out=unread[:],
+                    in_=zT[:, c, cols_a],
+                    func=ACT.Square,
+                    bias=neg_pivot[:, c : c + 1],
+                    scale=1.0,
+                    accum_out=squares[:, c, pair : pair + 1],
+                )
+                nc.vector.bn_stats(
+                    out=stats[:, c, 2 * pair : 2 * pair + 2, :].rearrange("p a s -> p (a s)"), in_=zT[:, c, cols_b]
+                )
+
+            blocks = [(pair, c) for pair in range(N_PAIRS) for c in range(K_BLOCKS)]
+            for n in range(len(blocks)):
+                pair, c = blocks[n]
+                if c == 0:
+                    load_pair(pair)
+                if (pair, c) == (1, 0):
                     nc.sync.dma_start(out=w_rows[:], in_=Wb1.rearrange("(a p) k -> p a k", p=P))
                     nc.gpsimd.tensor_scalar(
                         out=w_two[:], in0=w_rows[:], scalar1=0.0, scalar2=2.0, op0=ALU.is_ge, op1=ALU.mult
                     )
-                for c in range(K_BLOCKS):
-                    feats = slice(c * P, (c + 1) * P)
-                    turned_a = turn_ps.tile([P, ROW_TILES, P], BF16)
-                    for j in range(ROW_TILES):
-                        nc.tensor.transpose(turned_a[:, j, :], rows_a[:, j, feats], ident[:])
-                    turned_b = turn_ps.tile([P, ROW_TILES, P], BF16)
-                    for j in range(ROW_TILES):
-                        nc.tensor.transpose(turned_b[:, j, :], rows_b[:, j, feats], ident[:])
-                    nc.vector.tensor_scalar(
-                        out=zT[:, c, cols_a],
-                        in0=turned_a[:].rearrange("p j r -> p (j r)"),
-                        scalar1=1.0,
-                        scalar2=None,
-                        op0=ALU.mult,
-                        op1=ALU.add,
-                        accum_out=sums[:, c, pair : pair + 1],
-                    )
-                    nc.scalar.copy(out=zT[:, c, cols_b], in_=turned_b[:].rearrange("p j r -> p (j r)"))
-                    if pair == 0:
-                        nc.vector.tensor_scalar_mul(
-                            out=neg_pivot[:, c : c + 1], in0=sums[:, c, 0:1], scalar1=-1.0 / CHUNK
-                        )
-                    unread = waste.tile([P, CHUNK], BF16)
-                    nc.scalar.activation(
-                        out=unread[:],
-                        in_=zT[:, c, cols_a],
-                        func=ACT.Square,
-                        bias=neg_pivot[:, c : c + 1],
-                        scale=1.0,
-                        accum_out=squares[:, c, pair : pair + 1],
-                    )
-                    nc.vector.bn_stats(
-                        out=stats[:, c, 2 * pair : 2 * pair + 2, :].rearrange("p a s -> p (a s)"), in_=zT[:, c, cols_b]
-                    )
+                turn(pair, c)
+                if n > 0:
+                    measure(*blocks[n - 1])
+            measure(*blocks[-1])
 
             w_grouped = setup.tile([P, PASSES, OUTS, PACK], BF16, align_bytes=64)
 
@@ -169,9 +192,10 @@ def tile_binarymlp_pa_t_kernel(tc, z0, g0, beta0, Wb1, bb1, out):
             nc.vector.tensor_mul(out=mean_gain[:], in0=mean_var[:, :, 0], in1=gain[:])
             nc.vector.tensor_sub(out=shift[:], in0=vec_cols[:, K_BLOCKS : 2 * K_BLOCKS], in1=mean_gain[:])
 
-            def normalise(i):
-                cols = slice(i * CHUNK, (i + 1) * CHUNK)
-                for c in range(K_BLOCKS):
+            def normalise(first, count):
+                for piece in range(first, min(first + count, PIECES)):
+                    c = piece % K_BLOCKS
+                    cols = slice((piece // K_BLOCKS) * WIDE, (piece // K_BLOCKS + 1) * WIDE)
                     nc.vector.tensor_scalar(
                         out=zT[:, c, cols],
                         in0=zT[:, c, cols],
@@ -181,17 +205,18 @@ def tile_binarymlp_pa_t_kernel(tc, z0, g0, beta0, Wb1, bb1, out):
                         op1=ALU.add,
                     )
 
-            normalise(0)
-            normalise(1)
+            normalise(0, PIECES_AHEAD)
             nc.vector.quantize_mx(
                 out=w_codes[:].rearrange("p g n -> p (g n)").bitcast(FP8X4),
                 scales=w_scales[:].rearrange("p g n -> p (g n)"),
                 in_=w_grouped[:].rearrange("p g n t -> p (g n t)"),
             )
 
-        with tc.tile_pool(name="group", bufs=3) as group, tc.tile_pool(name="mx", bufs=3) as mx, tc.tile_pool(
-            name="res", bufs=3
-        ) as res, tc.psum_pool(name="acc_ps", bufs=8) as acc_ps:
+        with tc.tile_pool(name="group", bufs=3, reuse_waits="tile") as group, tc.tile_pool(
+            name="mx", bufs=3, reuse_waits="tile"
+        ) as mx, tc.tile_pool(name="res", bufs=3, reuse_waits="tile") as res, tc.psum_pool(
+            name="acc_ps", bufs=8, reuse_waits="tile"
+        ) as acc_ps:
             grouped = {}
             h_codes = {}
             h_scales = {}
@@ -240,12 +265,14 @@ def tile_binarymlp_pa_t_kernel(tc, z0, g0, beta0, Wb1, bb1, out):
                     nc.vector.tensor_tensor(out=result[:, j, :], in0=accs[j][:], in1=bias_all[:], op=ALU.add)
                 nc.sync.dma_start(out=out[cols, :].rearrange("(p j) n -> p j n", j=ROW_TILES), in_=result[:])
 
+            accs = {}
             regroup(0)
             for i in range(N_CHUNKS):
                 if i + 1 < N_CHUNKS:
                     regroup(i + 1)
                 quantise(i)
-                accs = multiply(i)
-                if i + 2 < N_CHUNKS:
-                    normalise(i + 2)
-                finish(i, accs)
+                accs[i] = multiply(i)
+                normalise(PIECES_AHEAD + i * PIECES_A_STEP, PIECES_A_STEP)
+                if i > 0:
+                    finish(i - 1, accs[i - 1])
+            finish(N_CHUNKS - 1, accs[N_CHUNKS - 1])

@@ -25,6 +25,7 @@ N_CHUNKS = BATCH // CHUNK
 N_PAIRS = N_CHUNKS // 2
 TRIPLES = 2 * N_PAIRS + 1
 SUMMED = N_PAIRS * CHUNK
+SUM_COLS = 64
 WIDE = 4 * CHUNK
 PIECES = K_BLOCKS * (BATCH // WIDE)
 PIECES_A_STEP = PIECES // N_CHUNKS
@@ -78,6 +79,7 @@ def tile_binarymlp_pa_t_kernel(tc, z0, g0, beta0, Wb1, bb1, out):
             w_two = setup.tile([P, OUT_TILES, FEATS], BF16)
             rows_a = {}
             rows_b = {}
+            sum_ps = {}
 
             def columns(pair):
                 first = 2 * pair * CHUNK
@@ -96,21 +98,25 @@ def tile_binarymlp_pa_t_kernel(tc, z0, g0, beta0, Wb1, bb1, out):
                 turned_a = turn_ps.tile([P, ROW_TILES, P], BF16)
                 for j in range(ROW_TILES):
                     nc.tensor.transpose(turned_a[:, j, :], rows_a[pair][:, j, feats], ident[:])
+                if c == 0:
+                    sum_ps[pair] = setup_ps.tile([P, K_BLOCKS, SUM_COLS], FP32, tag="setup", name="sum_ps")
+                for j in range(ROW_TILES):
+                    nc.tensor.matmul(
+                        out=sum_ps[pair][:, c, :],
+                        lhsT=rows_a[pair][:, j, feats],
+                        rhs=ones[:, 0:SUM_COLS],
+                        start=(j == 0),
+                        stop=(j == ROW_TILES - 1),
+                    )
                 turned_b = turn_ps.tile([P, ROW_TILES, P], BF16)
                 for j in range(ROW_TILES):
                     nc.tensor.transpose(turned_b[:, j, :], rows_b[pair][:, j, feats], ident[:])
-                nc.vector.tensor_scalar(
-                    out=zT[:, c, cols_a],
-                    in0=turned_a[:].rearrange("p j r -> p (j r)"),
-                    scalar1=1.0,
-                    scalar2=None,
-                    op0=ALU.mult,
-                    op1=ALU.add,
-                    accum_out=sums[:, c, pair : pair + 1],
-                )
+                nc.vector.tensor_copy(out=zT[:, c, cols_a], in_=turned_a[:].rearrange("p j r -> p (j r)"))
                 nc.scalar.copy(out=zT[:, c, cols_b], in_=turned_b[:].rearrange("p j r -> p (j r)"))
                 if pair == 0:
-                    nc.vector.tensor_scalar_mul(out=neg_pivot[:, c : c + 1], in0=sums[:, c, 0:1], scalar1=-1.0 / CHUNK)
+                    nc.vector.tensor_scalar_mul(out=neg_pivot[:, c : c + 1], in0=zT[:, c, 0:1], scalar1=-1.0)
+                if c == K_BLOCKS - 1:
+                    nc.vector.tensor_copy(out=sums[:, :, pair], in_=sum_ps[pair][:, :, 0])
 
             def measure(pair, c):
                 cols_a, cols_b = columns(pair)

@@ -27,9 +27,10 @@ TRIPLES = 2 * N_PAIRS + 1
 SUMMED = N_PAIRS * CHUNK
 SUM_COLS = 64
 WIDE = 4 * CHUNK
-PIECES = K_BLOCKS * (BATCH // WIDE)
-PIECES_A_STEP = PIECES // N_CHUNKS
-PIECES_AHEAD = K_BLOCKS + PIECES_A_STEP
+SPANS = 1 + (BATCH - CHUNK + WIDE - 1) // WIDE
+PIECES = K_BLOCKS * SPANS
+PIECES_A_STEP = K_BLOCKS * CHUNK // WIDE
+PIECES_AHEAD = 2 * K_BLOCKS
 
 
 def tile_binarymlp_pa_t_kernel(tc, z0, g0, beta0, Wb1, bb1, out):
@@ -44,23 +45,23 @@ def tile_binarymlp_pa_t_kernel(tc, z0, g0, beta0, Wb1, bb1, out):
         gain = keep.tile([P, K_BLOCKS], FP32)
         shift = keep.tile([P, K_BLOCKS], FP32)
 
-        one = keep.tile([P, 1], FP32)
-        nc.vector.memset(one[:], 1.0)
-        warm = keep.tile([P, 1], FP32)
-        nc.scalar.sqrt(out=warm[:], in_=one[:])
-
         with tc.tile_pool(name="load", bufs=3) as load, tc.tile_pool(name="waste", bufs=4) as waste, tc.tile_pool(
             name="setup", bufs=1
         ) as setup, tc.psum_pool(name="turn_ps", bufs=3) as turn_ps, tc.psum_pool(name="setup_ps", bufs=2) as setup_ps:
             vec_rows = setup.tile([P, P], BF16)
             nc.vector.memset(vec_rows[:], 0.0)
-            nc.sync.dma_start(out=vec_rows[0:K_BLOCKS, :], in_=g0.rearrange("(c p) -> c p", p=P))
-            nc.sync.dma_start(out=vec_rows[K_BLOCKS : 2 * K_BLOCKS, :], in_=beta0.rearrange("(c p) -> c p", p=P))
+            nc.scalar.dma_start(out=vec_rows[0:K_BLOCKS, :], in_=g0.rearrange("(c p) -> c p", p=P))
+            nc.scalar.dma_start(out=vec_rows[K_BLOCKS : 2 * K_BLOCKS, :], in_=beta0.rearrange("(c p) -> c p", p=P))
             bias_row = setup.tile([P, OUTS], BF16)
             nc.vector.memset(bias_row[:], 0.0)
-            nc.sync.dma_start(out=bias_row[0:1, :], in_=bb1.rearrange("(o n) -> o n", o=1))
+            nc.scalar.dma_start(out=bias_row[0:1, :], in_=bb1.rearrange("(o n) -> o n", o=1))
             ones = setup.tile([P, P], BF16)
             nc.vector.memset(ones[:], 1.0)
+
+            one = setup.tile([P, 1], FP32)
+            nc.vector.memset(one[:], 1.0)
+            warm = setup.tile([P, 1], FP32)
+            nc.scalar.sqrt(out=warm[:], in_=one[:])
 
             vec_ps = setup_ps.tile([P, P], BF16, tag="setup")
             nc.tensor.transpose(vec_ps[:], vec_rows[:], ident[:])
@@ -114,7 +115,9 @@ def tile_binarymlp_pa_t_kernel(tc, z0, g0, beta0, Wb1, bb1, out):
                 nc.vector.tensor_copy(out=zT[:, c, cols_a], in_=turned_a[:].rearrange("p j r -> p (j r)"))
                 nc.scalar.copy(out=zT[:, c, cols_b], in_=turned_b[:].rearrange("p j r -> p (j r)"))
                 if pair == 0:
-                    nc.vector.tensor_scalar_mul(out=neg_pivot[:, c : c + 1], in0=zT[:, c, 0:1], scalar1=-1.0)
+                    nc.vector.tensor_scalar_mul(
+                        out=neg_pivot[:, c : c + 1], in0=sum_ps[pair][:, c, 0:1], scalar1=-1.0 / CHUNK
+                    )
                 if c == K_BLOCKS - 1:
                     nc.vector.tensor_copy(out=sums[:, :, pair], in_=sum_ps[pair][:, :, 0])
 
@@ -201,7 +204,8 @@ def tile_binarymlp_pa_t_kernel(tc, z0, g0, beta0, Wb1, bb1, out):
             def normalise(first, count):
                 for piece in range(first, min(first + count, PIECES)):
                     c = piece % K_BLOCKS
-                    cols = slice((piece // K_BLOCKS) * WIDE, (piece // K_BLOCKS + 1) * WIDE)
+                    span = piece // K_BLOCKS
+                    cols = slice(max(0, CHUNK + (span - 1) * WIDE), min(CHUNK + span * WIDE, BATCH))
                     nc.vector.tensor_scalar(
                         out=zT[:, c, cols],
                         in0=zT[:, c, cols],
@@ -266,10 +270,15 @@ def tile_binarymlp_pa_t_kernel(tc, z0, g0, beta0, Wb1, bb1, out):
 
             def finish(i, accs):
                 cols = slice(i * CHUNK, (i + 1) * CHUNK)
+                out_rows = out[cols, :].rearrange("(p j) n -> p j n", j=ROW_TILES)
+                last = i == N_CHUNKS - 1
                 result = res.tile([P, ROW_TILES, OUTS], FP32)
                 for j in range(ROW_TILES):
                     nc.vector.tensor_tensor(out=result[:, j, :], in0=accs[j][:], in1=bias_all[:], op=ALU.add)
-                nc.sync.dma_start(out=out[cols, :].rearrange("(p j) n -> p j n", j=ROW_TILES), in_=result[:])
+                    if last:
+                        nc.sync.dma_start(out=out_rows[:, j, :], in_=result[:, j, :])
+                if not last:
+                    nc.sync.dma_start(out=out_rows, in_=result[:])
 
             accs = {}
             regroup(0)

@@ -16,42 +16,95 @@ BATCH, FEATS, OUTS = 8192, 1024, 512
 BN_EPS = 1e-5
 FLOPS = 2 * BATCH * FEATS * OUTS
 
-K_BLOCKS = FEATS // P
-PASSES = K_BLOCKS // PACK
+PASSES = 2
+HALF = FEATS // PASSES
+BLOCKS = HALF // P
 OUT_TILES = OUTS // P
 ROW_TILES = 4
 CHUNK = ROW_TILES * P
 N_CHUNKS = BATCH // CHUNK
-N_PAIRS = N_CHUNKS // 2
-TRIPLES = 2 * N_PAIRS + 1
-SUMMED = N_PAIRS * CHUNK
+QUAD = 4
+QUAD_COLS = QUAD * CHUNK
+N_QUADS = N_CHUNKS // QUAD
 SUM_COLS = 64
-WIDE = 4 * CHUNK
-SPANS = 1 + (BATCH - CHUNK + WIDE - 1) // WIDE
-PIECES = K_BLOCKS * SPANS
-PIECES_A_STEP = K_BLOCKS * CHUNK // WIDE
-PIECES_AHEAD = 2 * K_BLOCKS
+LOADS_AHEAD = 8
+LAG = 3
+START = 2
 
 
 def tile_binarymlp_pa_t_kernel(tc, z0, g0, beta0, Wb1, bb1, out):
     nc = tc.nc
-    with tc.manual_schedule(), tc.tile_pool(name="keep", bufs=1) as keep:
+    with tc.manual_schedule(), tc.tile_pool(name="keep", bufs=1) as keep, tc.tile_pool(
+        name="quads", bufs=N_QUADS + 2
+    ) as quads, tc.tile_pool(name="group", bufs=3) as group:
         ident = keep.tile([P, P], BF16)
         make_identity(nc, ident[:])
-        zT = keep.tile([P, K_BLOCKS, BATCH], BF16)
         w_codes = keep.tile([P, PASSES, OUTS], U32, align_bytes=64)
         w_scales = keep.tile([P, PASSES, OUTS], U8, align_bytes=64)
+        h_codes_0 = keep.tile([P, N_CHUNKS, CHUNK], U32, align_bytes=64)
+        h_scales_0 = keep.tile([P, N_CHUNKS, CHUNK], U8, align_bytes=64)
         bias_all = keep.tile([P, OUTS], FP32)
-        gain = keep.tile([P, K_BLOCKS], FP32)
-        shift = keep.tile([P, K_BLOCKS], FP32)
+        gain = keep.tile([P, PASSES, BLOCKS], FP32)
+        shift = keep.tile([P, PASSES, BLOCKS], FP32)
+        zT = {}
+        grouped = {}
+        h_codes_1 = {}
+        h_scales_1 = {}
 
-        with tc.tile_pool(name="load", bufs=3) as load, tc.tile_pool(name="waste", bufs=4) as waste, tc.tile_pool(
+        def turned_cols(half, i, c):
+            first = (i % QUAD) * CHUNK
+            return zT[half, i // QUAD][:, c, first : first + CHUNK]
+
+        def normalise(half, quad, c, first, count, engine):
+            piece = zT[half, quad][:, c, first : first + count]
+            engine.tensor_scalar(
+                out=piece,
+                in0=piece,
+                scalar1=gain[:, half, c : c + 1],
+                scalar2=shift[:, half, c : c + 1],
+                op0=ALU.mult,
+                op1=ALU.add,
+            )
+
+        def regroup(half, i, on_vector):
+            grouped[half, i] = group.tile([P, CHUNK, PACK], BF16, align_bytes=64, name="grouped")
+            first = (i % QUAD) * CHUNK
+            dst = grouped[half, i][:].rearrange("p (q i) t -> p q t i", i=4)
+            src = zT[half, i // QUAD][:, :, first : first + CHUNK].rearrange("p t (q i) -> p q t i", i=4)
+            if on_vector:
+                nc.vector.tensor_scalar_max(out=dst, in0=src, scalar1=0.0)
+            else:
+                nc.scalar.activation(out=dst, in_=src, func=ACT.Relu)
+
+        def quantise_into(half, i, codes, scales):
+            nc.vector.quantize_mx(
+                out=codes.bitcast(FP8X4), scales=scales, in_=grouped[half, i][:].rearrange("p w t -> p (w t)")
+            )
+
+        def quantise_0(i):
+            quantise_into(0, i, h_codes_0[:, i, :], h_scales_0[:, i, :])
+
+        with tc.tile_pool(name="load", bufs=LOADS_AHEAD) as load, tc.tile_pool(name="waste", bufs=4) as waste, tc.tile_pool(
             name="setup", bufs=1
-        ) as setup, tc.psum_pool(name="turn_ps", bufs=3) as turn_ps, tc.psum_pool(name="setup_ps", bufs=2) as setup_ps:
+        ) as setup, tc.psum_pool(name="turn_ps", bufs=6) as turn_ps, tc.psum_pool(name="sum_ps", bufs=2) as small_ps:
+            rows = {}
+
+            def load_chunk(n):
+                half, i = n // N_CHUNKS, n % N_CHUNKS
+                rows[half, i] = load.tile([P, ROW_TILES, HALF], BF16, name="rows")
+                src = z0[i * CHUNK : (i + 1) * CHUNK, half * HALF : (half + 1) * HALF]
+                nc.sync.dma_start(out=rows[half, i][:], in_=src.rearrange("(p j) f -> p j f", j=ROW_TILES))
+
+            for n in range(LOADS_AHEAD):
+                load_chunk(n)
+            w_rows = setup.tile([P, OUT_TILES, FEATS], BF16)
+            nc.sync.dma_start(out=w_rows[:], in_=Wb1.rearrange("(a p) k -> p a k", p=P))
+
             vec_rows = setup.tile([P, P], BF16)
             nc.vector.memset(vec_rows[:], 0.0)
-            nc.scalar.dma_start(out=vec_rows[0:K_BLOCKS, :], in_=g0.rearrange("(c p) -> c p", p=P))
-            nc.scalar.dma_start(out=vec_rows[K_BLOCKS : 2 * K_BLOCKS, :], in_=beta0.rearrange("(c p) -> c p", p=P))
+            n_vec = FEATS // P
+            nc.scalar.dma_start(out=vec_rows[0:n_vec, :], in_=g0.rearrange("(c p) -> c p", p=P))
+            nc.scalar.dma_start(out=vec_rows[n_vec : 2 * n_vec, :], in_=beta0.rearrange("(c p) -> c p", p=P))
             bias_row = setup.tile([P, OUTS], BF16)
             nc.vector.memset(bias_row[:], 0.0)
             nc.scalar.dma_start(out=bias_row[0:1, :], in_=bb1.rearrange("(o n) -> o n", o=1))
@@ -63,203 +116,235 @@ def tile_binarymlp_pa_t_kernel(tc, z0, g0, beta0, Wb1, bb1, out):
             warm = setup.tile([P, 1], FP32)
             nc.scalar.sqrt(out=warm[:], in_=one[:])
 
-            vec_ps = setup_ps.tile([P, P], BF16, tag="setup")
-            nc.tensor.transpose(vec_ps[:], vec_rows[:], ident[:])
-            vec_cols = setup.tile([P, 2 * K_BLOCKS], FP32)
-            nc.vector.tensor_copy(out=vec_cols[:], in_=vec_ps[:, 0 : 2 * K_BLOCKS])
-            bias_ps = setup_ps.tile([P, OUTS], FP32, tag="setup")
-            nc.tensor.matmul(out=bias_ps[:], lhsT=ones[:], rhs=bias_row[:], start=True, stop=True)
-            nc.vector.tensor_copy(out=bias_all[:], in_=bias_ps[:])
+            vec_cols = setup.tile([P, 2, PASSES, BLOCKS], FP32)
 
-            stats = setup.tile([P, K_BLOCKS, TRIPLES, 3], FP32)
-            nc.vector.memset(stats[:, :, TRIPLES - 1, 0:1], float(SUMMED))
-            sums = setup.tile([P, K_BLOCKS, N_PAIRS], FP32)
-            squares = setup.tile([P, K_BLOCKS, N_PAIRS], FP32)
-            neg_pivot = setup.tile([P, K_BLOCKS], FP32)
-            w_rows = setup.tile([P, OUT_TILES, FEATS], BF16)
-            w_two = setup.tile([P, OUT_TILES, FEATS], BF16)
-            rows_a = {}
-            rows_b = {}
-            sum_ps = {}
+            def spread_vectors():
+                vec_ps = small_ps.tile([P, P], BF16, tag="small")
+                nc.tensor.transpose(vec_ps[:], vec_rows[:], ident[:])
+                nc.vector.tensor_copy(
+                    out=vec_cols[:].rearrange("p v h c -> p (v h c)"), in_=vec_ps[:, 0 : 2 * n_vec]
+                )
+                bias_ps = small_ps.tile([P, OUTS], FP32, tag="small")
+                nc.tensor.matmul(out=bias_ps[:], lhsT=ones[:], rhs=bias_row[:], start=True, stop=True)
+                nc.vector.tensor_copy(out=bias_all[:], in_=bias_ps[:])
 
-            def columns(pair):
-                first = 2 * pair * CHUNK
-                return slice(first, first + CHUNK), slice(first + CHUNK, first + 2 * CHUNK)
+            neg_pivot = setup.tile([P, PASSES, BLOCKS], FP32)
+            sums = setup.tile([P, PASSES, BLOCKS, N_CHUNKS], FP32)
+            squares = setup.tile([P, PASSES, BLOCKS, N_CHUNKS], FP32)
+            sum_bank = {}
 
-            def load_pair(pair):
-                cols_a, cols_b = columns(pair)
-                rows_a[pair] = load.tile([P, ROW_TILES, FEATS], BF16, name="rows_a")
-                nc.sync.dma_start(out=rows_a[pair][:], in_=z0[cols_a, :].rearrange("(p j) f -> p j f", j=ROW_TILES))
-                rows_b[pair] = load.tile([P, ROW_TILES, FEATS], BF16, name="rows_b")
-                nc.sync.dma_start(out=rows_b[pair][:], in_=z0[cols_b, :].rearrange("(p j) f -> p j f", j=ROW_TILES))
-
-            def turn(pair, c):
-                cols_a, cols_b = columns(pair)
-                feats = slice(c * P, (c + 1) * P)
-                turned_a = turn_ps.tile([P, ROW_TILES, P], BF16)
+            def turn(half, i, c, on_vector):
+                if (half, i // QUAD) not in zT:
+                    zT[half, i // QUAD] = quads.tile([P, BLOCKS, QUAD_COLS], BF16, name="zT")
+                bank = turn_ps.tile([P, ROW_TILES, P], BF16, name="turned")
                 for j in range(ROW_TILES):
-                    nc.tensor.transpose(turned_a[:, j, :], rows_a[pair][:, j, feats], ident[:])
+                    nc.tensor.transpose(bank[:, j, :], rows[half, i][:, j, c * P : (c + 1) * P], ident[:])
+                flat = bank[:].rearrange("p j r -> p (j r)")
+                if on_vector:
+                    nc.vector.tensor_copy(out=turned_cols(half, i, c), in_=flat)
+                else:
+                    nc.scalar.copy(out=turned_cols(half, i, c), in_=flat)
+
+            def add_rows(half, i, c):
                 if c == 0:
-                    sum_ps[pair] = setup_ps.tile([P, K_BLOCKS, SUM_COLS], FP32, tag="setup", name="sum_ps")
+                    sum_bank[half, i] = small_ps.tile([P, BLOCKS, SUM_COLS], FP32, tag="small", name="sum_bank")
                 for j in range(ROW_TILES):
                     nc.tensor.matmul(
-                        out=sum_ps[pair][:, c, :],
-                        lhsT=rows_a[pair][:, j, feats],
+                        out=sum_bank[half, i][:, c, :],
+                        lhsT=rows[half, i][:, j, c * P : (c + 1) * P],
                         rhs=ones[:, 0:SUM_COLS],
                         start=(j == 0),
                         stop=(j == ROW_TILES - 1),
                     )
-                turned_b = turn_ps.tile([P, ROW_TILES, P], BF16)
-                for j in range(ROW_TILES):
-                    nc.tensor.transpose(turned_b[:, j, :], rows_b[pair][:, j, feats], ident[:])
-                nc.vector.tensor_copy(out=zT[:, c, cols_a], in_=turned_a[:].rearrange("p j r -> p (j r)"))
-                nc.scalar.copy(out=zT[:, c, cols_b], in_=turned_b[:].rearrange("p j r -> p (j r)"))
-                if pair == 0:
-                    nc.vector.tensor_scalar_mul(
-                        out=neg_pivot[:, c : c + 1], in0=sum_ps[pair][:, c, 0:1], scalar1=-1.0 / CHUNK
-                    )
-                if c == K_BLOCKS - 1:
-                    nc.vector.tensor_copy(out=sums[:, :, pair], in_=sum_ps[pair][:, :, 0])
 
-            def measure(pair, c):
-                cols_a, cols_b = columns(pair)
+            def keep_sums(half, i, column, c):
+                if i == 0:
+                    nc.vector.tensor_scalar_mul(
+                        out=neg_pivot[:, half, c : c + 1], in0=sum_bank[half, i][:, c, 0:1], scalar1=-1.0 / CHUNK
+                    )
+                if c == BLOCKS - 1:
+                    nc.vector.tensor_copy(out=sums[:, half, :, column], in_=sum_bank[half, i][:, :, 0])
+
+            def square(half, i, column, c):
                 unread = waste.tile([P, CHUNK], BF16)
                 nc.scalar.activation(
                     out=unread[:],
-                    in_=zT[:, c, cols_a],
+                    in_=turned_cols(half, i, c),
                     func=ACT.Square,
-                    bias=neg_pivot[:, c : c + 1],
+                    bias=neg_pivot[:, half, c : c + 1],
                     scale=1.0,
-                    accum_out=squares[:, c, pair : pair + 1],
-                )
-                nc.vector.bn_stats(
-                    out=stats[:, c, 2 * pair : 2 * pair + 2, :].rearrange("p a s -> p (a s)"), in_=zT[:, c, cols_b]
+                    accum_out=squares[:, half, c, column : column + 1],
                 )
 
-            blocks = [(pair, c) for pair in range(N_PAIRS) for c in range(K_BLOCKS)]
-            for n in range(len(blocks)):
-                pair, c = blocks[n]
-                if c == 0:
-                    load_pair(pair)
-                if (pair, c) == (1, 0):
-                    nc.sync.dma_start(out=w_rows[:], in_=Wb1.rearrange("(a p) k -> p a k", p=P))
+            pairs = N_CHUNKS // 2
+            triples = 2 * pairs + 1
+            stats = setup.tile([P, BLOCKS, triples, 3], FP32)
+            nc.vector.memset(stats[:, :, triples - 1, 0:1], float(pairs * CHUNK))
+
+            def measure_pair(pair, c):
+                square(0, 2 * pair, pair, c)
+                nc.vector.bn_stats(
+                    out=stats[:, c, 2 * pair : 2 * pair + 2, :].rearrange("p a s -> p (a s)"),
+                    in_=turned_cols(0, 2 * pair + 1, c),
+                )
+
+            before = None
+            for pair in range(pairs):
+                for c in range(BLOCKS):
+                    turn(0, 2 * pair, c, True)
+                    add_rows(0, 2 * pair, c)
+                    turn(0, 2 * pair + 1, c, False)
+                    keep_sums(0, 2 * pair, pair, c)
+                    if before is not None:
+                        measure_pair(*before)
+                    before = (pair, c)
+                load_chunk(LOADS_AHEAD + 2 * pair)
+                load_chunk(LOADS_AHEAD + 2 * pair + 1)
+                if pair == 2:
+                    w_two = setup.tile([P, OUT_TILES, FEATS], BF16)
                     nc.gpsimd.tensor_scalar(
                         out=w_two[:], in0=w_rows[:], scalar1=0.0, scalar2=2.0, op0=ALU.is_ge, op1=ALU.mult
                     )
-                turn(pair, c)
-                if n > 0:
-                    measure(*blocks[n - 1])
-            measure(*blocks[-1])
+                    spread_vectors()
+            measure_pair(*before)
+
+            mean_var = setup.tile([P, PASSES, BLOCKS, 2], FP32)
+            var_eps = setup.tile([P, PASSES, BLOCKS], FP32)
+            std = setup.tile([P, PASSES, BLOCKS], FP32)
+
+            def sum_up(half, columns, mean, spread):
+                count = float(columns * CHUNK)
+                total = setup.tile([P, BLOCKS], FP32, name=f"total{half}")
+                nc.vector.tensor_reduce(out=total[:], in_=sums[:, half, :, 0:columns], axis=AXIS.X, op=ALU.add)
+                square_total = setup.tile([P, BLOCKS], FP32, name=f"square_total{half}")
+                nc.vector.tensor_reduce(
+                    out=square_total[:], in_=squares[:, half, :, 0:columns], axis=AXIS.X, op=ALU.add
+                )
+                nc.vector.tensor_scalar_mul(out=mean, in0=total[:], scalar1=1.0 / count)
+                off = setup.tile([P, BLOCKS], FP32, name=f"off{half}")
+                nc.vector.tensor_add(out=off[:], in0=mean, in1=neg_pivot[:, half, :])
+                off_sq = setup.tile([P, BLOCKS], FP32, name=f"off_sq{half}")
+                nc.vector.tensor_mul(out=off_sq[:], in0=off[:], in1=off[:])
+                nc.vector.scalar_tensor_tensor(
+                    out=spread, in0=off_sq[:], scalar=-count, in1=square_total[:], op0=ALU.mult, op1=ALU.add
+                )
+
+            def variance_0():
+                sum_up(0, pairs, stats[:, :, triples - 1, 1], stats[:, :, triples - 1, 2])
+                for c in range(BLOCKS):
+                    nc.vector.bn_aggr(out=mean_var[:, 0, c, :], in_=stats[:, c, :, :].rearrange("p a s -> p (a s)"))
+                nc.vector.tensor_scalar_add(out=var_eps[:, 0, :], in0=mean_var[:, 0, :, 1], scalar1=BN_EPS)
+
+            def variance_1():
+                spread = setup.tile([P, BLOCKS], FP32, name="spread1")
+                sum_up(1, N_CHUNKS, mean_var[:, 1, :, 0], spread[:])
+                nc.vector.tensor_scalar(
+                    out=var_eps[:, 1, :], in0=spread[:], scalar1=1.0 / BATCH, scalar2=BN_EPS, op0=ALU.mult, op1=ALU.add
+                )
+
+            def gain_and_shift(half):
+                rstd = setup.tile([P, BLOCKS], FP32, name=f"rstd{half}")
+                nc.vector.reciprocal(out=rstd[:], in_=std[:, half, :])
+                nc.vector.tensor_mul(out=gain[:, half, :], in0=vec_cols[:, 0, half, :], in1=rstd[:])
+                mean_gain = setup.tile([P, BLOCKS], FP32, name=f"mean_gain{half}")
+                nc.vector.tensor_mul(out=mean_gain[:], in0=mean_var[:, half, :, 0], in1=gain[:, half, :])
+                nc.vector.tensor_sub(out=shift[:, half, :], in0=vec_cols[:, 1, half, :], in1=mean_gain[:])
 
             w_grouped = setup.tile([P, PASSES, OUTS, PACK], BF16, align_bytes=64)
 
-            def turn_weights(g):
-                for a in range(OUT_TILES):
-                    w_ps = setup_ps.tile([P, PACK, P], BF16, tag="setup")
-                    for t in range(PACK):
-                        c = PACK * g + t
-                        nc.tensor.transpose(w_ps[:, t, :], w_two[:, a, c * P : (c + 1) * P], ident[:])
-                    nc.scalar.activation(
-                        out=w_grouped[:, g, a * P : (a + 1) * P, :],
-                        in_=w_ps[:].rearrange("p t n -> p n t"),
-                        func=ACT.Copy,
-                        bias=-1.0,
-                        scale=1.0,
-                    )
-
-            turn_weights(0)
-            sum_a = setup.tile([P, K_BLOCKS], FP32)
-            nc.vector.tensor_reduce(out=sum_a[:], in_=sums[:], axis=AXIS.X, op=ALU.add)
-            square_a = setup.tile([P, K_BLOCKS], FP32)
-            nc.vector.tensor_reduce(out=square_a[:], in_=squares[:], axis=AXIS.X, op=ALU.add)
-            mean_a = stats[:, :, TRIPLES - 1, 1]
-            nc.vector.tensor_scalar_mul(out=mean_a, in0=sum_a[:], scalar1=1.0 / SUMMED)
-            off = setup.tile([P, K_BLOCKS], FP32)
-            nc.vector.tensor_add(out=off[:], in0=mean_a, in1=neg_pivot[:])
-            off_sq = setup.tile([P, K_BLOCKS], FP32)
-            nc.vector.tensor_mul(out=off_sq[:], in0=off[:], in1=off[:])
-            nc.vector.scalar_tensor_tensor(
-                out=stats[:, :, TRIPLES - 1, 2],
-                in0=off_sq[:],
-                scalar=-float(SUMMED),
-                in1=square_a[:],
-                op0=ALU.mult,
-                op1=ALU.add,
-            )
-            mean_var = setup.tile([P, K_BLOCKS, 2], FP32)
-            for c in range(K_BLOCKS):
-                nc.vector.bn_aggr(out=mean_var[:, c, :], in_=stats[:, c, :, :].rearrange("p a s -> p (a s)"))
-            var_eps = setup.tile([P, K_BLOCKS], FP32)
-            nc.vector.tensor_scalar_add(out=var_eps[:], in0=mean_var[:, :, 1], scalar1=BN_EPS)
-            std = setup.tile([P, K_BLOCKS], FP32)
-            nc.scalar.sqrt(out=std[:], in_=var_eps[:])
-            turn_weights(1)
-            rstd = setup.tile([P, K_BLOCKS], FP32)
-            nc.vector.reciprocal(out=rstd[:], in_=std[:])
-            nc.vector.tensor_mul(out=gain[:], in0=vec_cols[:, 0:K_BLOCKS], in1=rstd[:])
-            mean_gain = setup.tile([P, K_BLOCKS], FP32)
-            nc.vector.tensor_mul(out=mean_gain[:], in0=mean_var[:, :, 0], in1=gain[:])
-            nc.vector.tensor_sub(out=shift[:], in0=vec_cols[:, K_BLOCKS : 2 * K_BLOCKS], in1=mean_gain[:])
-
-            def normalise(first, count):
-                for piece in range(first, min(first + count, PIECES)):
-                    c = piece % K_BLOCKS
-                    span = piece // K_BLOCKS
-                    cols = slice(max(0, CHUNK + (span - 1) * WIDE), min(CHUNK + span * WIDE, BATCH))
-                    nc.vector.tensor_scalar(
-                        out=zT[:, c, cols],
-                        in0=zT[:, c, cols],
-                        scalar1=gain[:, c : c + 1],
-                        scalar2=shift[:, c : c + 1],
-                        op0=ALU.mult,
-                        op1=ALU.add,
-                    )
-
-            normalise(0, PIECES_AHEAD)
-            nc.vector.quantize_mx(
-                out=w_codes[:].rearrange("p g n -> p (g n)").bitcast(FP8X4),
-                scales=w_scales[:].rearrange("p g n -> p (g n)"),
-                in_=w_grouped[:].rearrange("p g n t -> p (g n t)"),
-            )
-
-        with tc.tile_pool(name="group", bufs=3, reuse_waits="tile") as group, tc.tile_pool(
-            name="mx", bufs=3, reuse_waits="tile"
-        ) as mx, tc.tile_pool(name="res", bufs=3, reuse_waits="tile") as res, tc.psum_pool(
-            name="acc_ps", bufs=8, reuse_waits="tile"
-        ) as acc_ps:
-            grouped = {}
-            h_codes = {}
-            h_scales = {}
-
-            def regroup(i):
-                cols = slice(i * CHUNK, (i + 1) * CHUNK)
-                grouped[i] = group.tile([P, PASSES, CHUNK, PACK], BF16, align_bytes=64, name="grouped")
-                for g in range(PASSES):
-                    nc.scalar.activation(
-                        out=grouped[i][:, g, :, :].rearrange("p (q i) t -> p q t i", i=4),
-                        in_=zT[:, PACK * g : PACK * (g + 1), cols].rearrange("p t (q i) -> p q t i", i=4),
-                        func=ACT.Relu,
-                    )
-
-            def quantise(i):
-                h_codes[i] = mx.tile([P, PASSES, CHUNK], U32, align_bytes=64, name="h_codes")
-                h_scales[i] = mx.tile([P, PASSES, CHUNK], U8, align_bytes=64, name="h_scales")
-                nc.vector.quantize_mx(
-                    out=h_codes[i][:].rearrange("p g w -> p (g w)").bitcast(FP8X4),
-                    scales=h_scales[i][:].rearrange("p g w -> p (g w)"),
-                    in_=grouped[i][:].rearrange("p g w t -> p (g w t)"),
+            def turn_weights(n):
+                h, a = n // OUT_TILES, n % OUT_TILES
+                bank = turn_ps.tile([P, PACK, P], BF16, name="turned")
+                for t in range(PACK):
+                    first = h * HALF + t * P
+                    nc.tensor.transpose(bank[:, t, :], w_two[:, a, first : first + P], ident[:])
+                nc.scalar.activation(
+                    out=w_grouped[:, h, a * P : (a + 1) * P, :],
+                    in_=bank[:].rearrange("p t n -> p n t"),
+                    func=ACT.Copy,
+                    bias=-1.0,
+                    scale=1.0,
                 )
+
+            def normalise_0(piece):
+                if 0 <= piece < N_QUADS * BLOCKS:
+                    normalise(0, piece // BLOCKS, piece % BLOCKS, 0, QUAD_COLS, nc.vector)
+
+            behind = None
+            for i in range(N_CHUNKS):
+                done = i - LAG
+                for c in range(BLOCKS):
+                    on_vector = i <= START or c % 2 == 0
+                    turn(1, i, c, on_vector)
+                    add_rows(1, i, c)
+                    keep_sums(1, i, i, c)
+                    if behind is not None:
+                        square(1, behind[0], behind[0], behind[1])
+                    behind = (i, c)
+                    if done >= 0 and c == 0:
+                        regroup(0, done, True)
+                    if done >= 0 and c == 2:
+                        quantise_0(done)
+                    if i > START and c == 1:
+                        normalise_0(BLOCKS + i - START - 1)
+                if LOADS_AHEAD + N_CHUNKS + i < 2 * N_CHUNKS:
+                    load_chunk(LOADS_AHEAD + N_CHUNKS + i)
+                if i == 0:
+                    variance_0()
+                if i == 1:
+                    nc.scalar.sqrt(out=std[:, 0, :], in_=var_eps[:, 0, :])
+                    gain_and_shift(0)
+                if i == START:
+                    for piece in range(BLOCKS):
+                        normalise_0(piece)
+                if 4 <= i < 4 + PASSES * OUT_TILES:
+                    turn_weights(i - 4)
+                if i == N_CHUNKS - 2:
+                    nc.vector.quantize_mx(
+                        out=w_codes[:].rearrange("p g n -> p (g n)").bitcast(FP8X4),
+                        scales=w_scales[:].rearrange("p g n -> p (g n)"),
+                        in_=w_grouped[:].rearrange("p g n t -> p (g n t)"),
+                    )
+            square(1, behind[0], behind[0], behind[1])
+
+            variance_1()
+            nc.scalar.sqrt(out=std[:, 1, :], in_=var_eps[:, 1, :])
+            gain_and_shift(1)
+            for i in range(N_CHUNKS - LAG, N_CHUNKS):
+                regroup(0, i, False)
+
+        with tc.tile_pool(name="mx", bufs=3, reuse_waits="tile") as mx, tc.tile_pool(
+            name="res", bufs=3, reuse_waits="tile"
+        ) as res, tc.psum_pool(name="acc_ps", bufs=8, reuse_waits="tile") as acc_ps:
+
+            pieces = [(0, c, 0, CHUNK) for c in range(BLOCKS)]
+            pieces += [(0, c, CHUNK, QUAD_COLS - CHUNK) for c in range(BLOCKS)]
+            pieces += [(quad, c, 0, QUAD_COLS) for quad in range(1, N_QUADS) for c in range(BLOCKS)]
+            ahead = 2 * BLOCKS + 2
+
+            def normalise_1(first, count):
+                for quad, c, col, width in pieces[first : first + count]:
+                    normalise(1, quad, c, col, width, nc.vector)
+
+            def quantise_1(i):
+                h_codes_1[i] = mx.tile([P, CHUNK], U32, align_bytes=64, name="h_codes_1")
+                h_scales_1[i] = mx.tile([P, CHUNK], U8, align_bytes=64, name="h_scales_1")
+                quantise_into(1, i, h_codes_1[i][:], h_scales_1[i][:])
 
             def multiply(i):
                 accs = []
                 for j in range(ROW_TILES):
-                    rows = slice(j * P, (j + 1) * P)
+                    cols = slice(j * P, (j + 1) * P)
                     acc = acc_ps.tile([P, OUTS], FP32)
+                    halves = [
+                        (h_codes_0[:, i, cols], h_scales_0[:, i, cols]),
+                        (h_codes_1[i][:, cols], h_scales_1[i][:, cols]),
+                    ]
                     for g in range(PASSES):
                         nc.tensor.matmul_mx(
                             out=acc[:],
-                            lhsT=h_codes[i][:, g, rows].bitcast(FP8X4),
-                            lhsT_scale=h_scales[i][:, g, rows],
+                            lhsT=halves[g][0].bitcast(FP8X4),
+                            lhsT_scale=halves[g][1],
                             rhs=w_codes[:, g, :].bitcast(FP8X4),
                             rhs_scale=w_scales[:, g, :],
                             start=(g == 0),
@@ -269,8 +354,7 @@ def tile_binarymlp_pa_t_kernel(tc, z0, g0, beta0, Wb1, bb1, out):
                 return accs
 
             def finish(i, accs):
-                cols = slice(i * CHUNK, (i + 1) * CHUNK)
-                out_rows = out[cols, :].rearrange("(p j) n -> p j n", j=ROW_TILES)
+                out_rows = out[i * CHUNK : (i + 1) * CHUNK, :].rearrange("(p j) n -> p j n", j=ROW_TILES)
                 last = i == N_CHUNKS - 1
                 result = res.tile([P, ROW_TILES, OUTS], FP32)
                 for j in range(ROW_TILES):
@@ -280,14 +364,18 @@ def tile_binarymlp_pa_t_kernel(tc, z0, g0, beta0, Wb1, bb1, out):
                 if not last:
                     nc.sync.dma_start(out=out_rows, in_=result[:])
 
+            normalise_1(0, BLOCKS)
+            for i in range(N_CHUNKS - LAG, N_CHUNKS):
+                quantise_0(i)
+            normalise_1(BLOCKS, ahead - BLOCKS)
             accs = {}
-            regroup(0)
+            regroup(1, 0, False)
             for i in range(N_CHUNKS):
                 if i + 1 < N_CHUNKS:
-                    regroup(i + 1)
-                quantise(i)
+                    regroup(1, i + 1, False)
+                quantise_1(i)
                 accs[i] = multiply(i)
-                normalise(PIECES_AHEAD + i * PIECES_A_STEP, PIECES_A_STEP)
+                normalise_1(ahead + i, 1)
                 if i > 0:
                     finish(i - 1, accs[i - 1])
             finish(N_CHUNKS - 1, accs[N_CHUNKS - 1])

@@ -26,9 +26,10 @@ N_CHUNKS = BATCH // CHUNK
 QUAD = 4
 QUAD_COLS = QUAD * CHUNK
 N_QUADS = N_CHUNKS // QUAD
-SUM_COLS = 64
+SUM_COLS = 16
 LOADS_AHEAD = 8
 LAG = 3
+COLS_1 = N_CHUNKS // 2 + N_QUADS // 2
 START = 2
 
 
@@ -86,7 +87,9 @@ def tile_binarymlp_pa_t_kernel(tc, z0, g0, beta0, Wb1, bb1, out):
 
         with tc.tile_pool(name="load", bufs=LOADS_AHEAD) as load, tc.tile_pool(name="waste", bufs=4) as waste, tc.tile_pool(
             name="setup", bufs=1
-        ) as setup, tc.psum_pool(name="turn_ps", bufs=6) as turn_ps, tc.psum_pool(name="sum_ps", bufs=2) as small_ps:
+        ) as setup, tc.psum_pool(name="turn_ps", bufs=5) as turn_ps, tc.psum_pool(name="sum_ps", bufs=2) as small_ps, tc.psum_pool(
+            name="gram_ps", bufs=1
+        ) as gram_ps:
             rows = {}
 
             def load_chunk(n):
@@ -132,6 +135,8 @@ def tile_binarymlp_pa_t_kernel(tc, z0, g0, beta0, Wb1, bb1, out):
             sums = setup.tile([P, PASSES, BLOCKS, N_CHUNKS], FP32)
             squares = setup.tile([P, PASSES, BLOCKS, N_CHUNKS], FP32)
             sum_bank = {}
+            part_mean = setup.tile([P, BLOCKS], FP32)
+            part_var = setup.tile([P, BLOCKS], FP32)
 
             def turn(half, i, c, on_vector):
                 if (half, i // QUAD) not in zT:
@@ -156,6 +161,13 @@ def tile_binarymlp_pa_t_kernel(tc, z0, g0, beta0, Wb1, bb1, out):
                         start=(j == 0),
                         stop=(j == ROW_TILES - 1),
                     )
+
+            def multiply_rows(quad, k, c, gram_bank, gram_sums):
+                for j in range(ROW_TILES):
+                    x = rows[1, QUAD * quad + k][:, j, c * P : (c + 1) * P]
+                    first, last = k == 0 and j == 0, k == QUAD - 1 and j == ROW_TILES - 1
+                    nc.tensor.matmul(out=gram_bank[:, c, :], lhsT=x, rhs=x, start=first, stop=last)
+                    nc.tensor.matmul(out=gram_sums[:, c, :], lhsT=x, rhs=ones[:, 0:SUM_COLS], start=first, stop=last)
 
             def keep_sums(half, i, column, c):
                 if i == 0:
@@ -200,9 +212,9 @@ def tile_binarymlp_pa_t_kernel(tc, z0, g0, beta0, Wb1, bb1, out):
                     before = (pair, c)
                 load_chunk(LOADS_AHEAD + 2 * pair)
                 load_chunk(LOADS_AHEAD + 2 * pair + 1)
-                if pair == 2:
+                if pair == 4:
                     w_two = setup.tile([P, OUT_TILES, FEATS], BF16)
-                    nc.gpsimd.tensor_scalar(
+                    nc.vector.tensor_scalar(
                         out=w_two[:], in0=w_rows[:], scalar1=0.0, scalar2=2.0, op0=ALU.is_ge, op1=ALU.mult
                     )
                     spread_vectors()
@@ -235,11 +247,55 @@ def tile_binarymlp_pa_t_kernel(tc, z0, g0, beta0, Wb1, bb1, out):
                     nc.vector.bn_aggr(out=mean_var[:, 0, c, :], in_=stats[:, c, :, :].rearrange("p a s -> p (a s)"))
                 nc.vector.tensor_scalar_add(out=var_eps[:, 0, :], in0=mean_var[:, 0, :, 1], scalar1=BN_EPS)
 
-            def variance_1():
-                spread = setup.tile([P, BLOCKS], FP32, name="spread1")
-                sum_up(1, N_CHUNKS, mean_var[:, 1, :, 0], spread[:])
+            def gather_1():
+                total = setup.tile([P, BLOCKS], FP32, name="total1")
+                nc.vector.tensor_reduce(out=total[:], in_=sums[:, 1, :, 0 : COLS_1 - 1], axis=AXIS.X, op=ALU.add)
+                nc.vector.tensor_scalar_mul(out=part_mean[:], in0=total[:], scalar1=1.0 / BATCH)
+                square_total = setup.tile([P, BLOCKS], FP32, name="square_total1")
+                nc.vector.tensor_reduce(
+                    out=square_total[:], in_=squares[:, 1, :, 0 : COLS_1 - 1], axis=AXIS.X, op=ALU.add
+                )
                 nc.vector.tensor_scalar(
-                    out=var_eps[:, 1, :], in0=spread[:], scalar1=1.0 / BATCH, scalar2=BN_EPS, op0=ALU.mult, op1=ALU.add
+                    out=part_var[:], in0=square_total[:], scalar1=1.0 / BATCH, scalar2=BN_EPS, op0=ALU.mult, op1=ALU.add
+                )
+
+            def about_pivot(out_, totals):
+                half_way = setup.tile([P, BLOCKS], FP32, name="half_way")
+                nc.vector.scalar_tensor_tensor(
+                    out=half_way[:], in0=neg_pivot[:, 1, :], scalar=0.5 * QUAD_COLS, in1=totals, op0=ALU.mult, op1=ALU.add
+                )
+                nc.vector.scalar_tensor_tensor(
+                    out=out_, in0=half_way[:], scalar=2.0, in1=neg_pivot[:, 1, :], op0=ALU.mult, op1=ALU.mult
+                )
+
+            def diagonal(bank, out_):
+                picked = setup.tile([P, BLOCKS, P], FP32, name="picked")
+                nc.vector.tensor_tensor(
+                    out=picked[:], in0=bank[:], in1=ident[:].unsqueeze(1).to_broadcast([P, BLOCKS, P]), op=ALU.mult
+                )
+                nc.vector.tensor_reduce(out=out_, in_=picked[:], axis=AXIS.X, op=ALU.add)
+
+            def variance_1(bank):
+                totals = sums[:, 1, :, COLS_1 - 1]
+                nc.vector.scalar_tensor_tensor(
+                    out=mean_var[:, 1, :, 0], in0=totals, scalar=1.0 / BATCH, in1=part_mean[:], op0=ALU.mult, op1=ALU.add
+                )
+                moved = setup.tile([P, BLOCKS], FP32, name="moved")
+                about_pivot(moved[:], totals)
+                off = setup.tile([P, BLOCKS], FP32, name="off1")
+                nc.vector.tensor_add(out=off[:], in0=mean_var[:, 1, :, 0], in1=neg_pivot[:, 1, :])
+                so_far = setup.tile([P, BLOCKS], FP32, name="so_far")
+                nc.vector.scalar_tensor_tensor(
+                    out=so_far[:], in0=moved[:], scalar=1.0 / BATCH, in1=part_var[:], op0=ALU.mult, op1=ALU.add
+                )
+                off_sq = setup.tile([P, BLOCKS], FP32, name="off_sq1")
+                nc.vector.tensor_mul(out=off_sq[:], in0=off[:], in1=off[:])
+                raw = setup.tile([P, BLOCKS], FP32, name="raw")
+                diagonal(bank, raw[:])
+                rest = setup.tile([P, BLOCKS], FP32, name="rest")
+                nc.vector.tensor_sub(out=rest[:], in0=so_far[:], in1=off_sq[:])
+                nc.vector.scalar_tensor_tensor(
+                    out=var_eps[:, 1, :], in0=raw[:], scalar=1.0 / BATCH, in1=rest[:], op0=ALU.mult, op1=ALU.add
                 )
 
             def gain_and_shift(half):
@@ -270,25 +326,54 @@ def tile_binarymlp_pa_t_kernel(tc, z0, g0, beta0, Wb1, bb1, out):
                 if 0 <= piece < N_QUADS * BLOCKS:
                     normalise(0, piece // BLOCKS, piece % BLOCKS, 0, QUAD_COLS, nc.vector)
 
-            behind = None
+            waiting = []
+            columns = 0
             for i in range(N_CHUNKS):
                 done = i - LAG
-                for c in range(BLOCKS):
-                    on_vector = i <= START or c % 2 == 0
-                    turn(1, i, c, on_vector)
-                    add_rows(1, i, c)
-                    keep_sums(1, i, i, c)
-                    if behind is not None:
-                        square(1, behind[0], behind[0], behind[1])
-                    behind = (i, c)
-                    if done >= 0 and c == 0:
+                quad, part = i // QUAD, i % QUAD
+                gram = quad % 2 == 1
+                if gram and part == 0:
+                    gram_bank = gram_ps.tile([P, BLOCKS, P], FP32, name="gram_bank")
+                    gram_sums = small_ps.tile([P, BLOCKS, SUM_COLS], FP32, tag="small", name="gram_sums")
+                for k in range(BLOCKS):
+                    if gram:
+                        turn(1, QUAD * quad + k, part, i <= START)
+                        multiply_rows(quad, k, part, gram_bank, gram_sums)
+                    else:
+                        turn(1, i, k, i <= START)
+                        add_rows(1, i, k)
+                        keep_sums(1, i, columns, k)
+                        waiting.append((i, columns, k))
+                    if k >= 2 and i > 0:
+                        for times in range(1 if i < 12 or k == 2 else 2):
+                            if waiting:
+                                square(1, *waiting.pop(0))
+                    if done >= 0 and k == 0:
                         regroup(0, done, True)
-                    if done >= 0 and c == 2:
+                    if done >= 0 and k == 2:
                         quantise_0(done)
-                    if i > START and c == 1:
+                    if i > START and k == 1:
                         normalise_0(BLOCKS + i - START - 1)
-                if LOADS_AHEAD + N_CHUNKS + i < 2 * N_CHUNKS:
-                    load_chunk(LOADS_AHEAD + N_CHUNKS + i)
+                if not gram:
+                    columns += 1
+                elif part == BLOCKS - 1:
+                    nc.vector.tensor_copy(out=sums[:, 1, :, columns], in_=gram_sums[:, :, 0])
+                    if columns < COLS_1 - 1:
+                        raw_1 = setup.tile([P, BLOCKS], FP32, name="raw_1")
+                        diagonal(gram_bank, raw_1[:])
+                        moved_1 = setup.tile([P, BLOCKS], FP32, name="moved_1")
+                        about_pivot(moved_1[:], sums[:, 1, :, columns])
+                        nc.vector.tensor_add(out=squares[:, 1, :, columns], in0=raw_1[:], in1=moved_1[:])
+                    columns += 1
+                if gram and part == BLOCKS - 1:
+                    first = QUAD * quad
+                elif gram:
+                    first = i + 1
+                else:
+                    first = i
+                for j in range(first, i + 1):
+                    if LOADS_AHEAD + N_CHUNKS + j < 2 * N_CHUNKS:
+                        load_chunk(LOADS_AHEAD + N_CHUNKS + j)
                 if i == 0:
                     variance_0()
                 if i == 1:
@@ -297,17 +382,19 @@ def tile_binarymlp_pa_t_kernel(tc, z0, g0, beta0, Wb1, bb1, out):
                 if i == START:
                     for piece in range(BLOCKS):
                         normalise_0(piece)
-                if 4 <= i < 4 + PASSES * OUT_TILES:
-                    turn_weights(i - 4)
-                if i == N_CHUNKS - 2:
+                if i < PASSES * OUT_TILES // 2:
+                    turn_weights(2 * i)
+                    turn_weights(2 * i + 1)
+                if i == 5:
                     nc.vector.quantize_mx(
                         out=w_codes[:].rearrange("p g n -> p (g n)").bitcast(FP8X4),
                         scales=w_scales[:].rearrange("p g n -> p (g n)"),
                         in_=w_grouped[:].rearrange("p g n t -> p (g n t)"),
                     )
-            square(1, behind[0], behind[0], behind[1])
+                if i == N_CHUNKS - 1:
+                    gather_1()
 
-            variance_1()
+            variance_1(gram_bank)
             nc.scalar.sqrt(out=std[:, 1, :], in_=var_eps[:, 1, :])
             gain_and_shift(1)
             for i in range(N_CHUNKS - LAG, N_CHUNKS):

@@ -24,12 +24,13 @@ ROW_TILES = 4
 CHUNK = ROW_TILES * P
 N_CHUNKS = BATCH // CHUNK
 QUAD = 4
-QUAD_COLS = QUAD * CHUNK
 N_QUADS = N_CHUNKS // QUAD
-SUM_COLS = 16
+SUM_COLS_0 = 64
+SUM_COLS_1 = 4
 LOADS_AHEAD = 8
 LAG = 3
-COLS_1 = N_CHUNKS // 2 + N_QUADS // 2
+SQUARED = 2
+GRAM_ROWS = (QUAD - SQUARED) * CHUNK * N_QUADS
 START = 2
 
 
@@ -37,7 +38,7 @@ def tile_binarymlp_pa_t_kernel(tc, z0, g0, beta0, Wb1, bb1, out):
     nc = tc.nc
     with tc.manual_schedule(), tc.tile_pool(name="keep", bufs=1) as keep, tc.tile_pool(
         name="quads", bufs=N_QUADS + 2
-    ) as quads, tc.tile_pool(name="group", bufs=3) as group:
+    ) as quads, tc.tile_pool(name="group", bufs=4) as group:
         ident = keep.tile([P, P], BF16)
         make_identity(nc, ident[:])
         w_codes = keep.tile([P, PASSES, OUTS], U32, align_bytes=64)
@@ -53,11 +54,10 @@ def tile_binarymlp_pa_t_kernel(tc, z0, g0, beta0, Wb1, bb1, out):
         h_scales_1 = {}
 
         def turned_cols(half, i, c):
-            first = (i % QUAD) * CHUNK
-            return zT[half, i // QUAD][:, c, first : first + CHUNK]
+            return zT[half, i // QUAD][:, i % QUAD, c, :]
 
         def normalise(half, quad, c, first, count, engine):
-            piece = zT[half, quad][:, c, first : first + count]
+            piece = zT[half, quad][:, first : first + count, c, :]
             engine.tensor_scalar(
                 out=piece,
                 in0=piece,
@@ -69,9 +69,8 @@ def tile_binarymlp_pa_t_kernel(tc, z0, g0, beta0, Wb1, bb1, out):
 
         def regroup(half, i, on_vector):
             grouped[half, i] = group.tile([P, CHUNK, PACK], BF16, align_bytes=64, name="grouped")
-            first = (i % QUAD) * CHUNK
             dst = grouped[half, i][:].rearrange("p (q i) t -> p q t i", i=4)
-            src = zT[half, i // QUAD][:, :, first : first + CHUNK].rearrange("p t (q i) -> p q t i", i=4)
+            src = zT[half, i // QUAD][:, i % QUAD, :, :].rearrange("p t (q i) -> p q t i", i=4)
             if on_vector:
                 nc.vector.tensor_scalar_max(out=dst, in0=src, scalar1=0.0)
             else:
@@ -134,13 +133,12 @@ def tile_binarymlp_pa_t_kernel(tc, z0, g0, beta0, Wb1, bb1, out):
             neg_pivot = setup.tile([P, PASSES, BLOCKS], FP32)
             sums = setup.tile([P, PASSES, BLOCKS, N_CHUNKS], FP32)
             squares = setup.tile([P, PASSES, BLOCKS, N_CHUNKS], FP32)
-            sum_bank = {}
             part_mean = setup.tile([P, BLOCKS], FP32)
             part_var = setup.tile([P, BLOCKS], FP32)
 
             def turn(half, i, c, on_vector):
                 if (half, i // QUAD) not in zT:
-                    zT[half, i // QUAD] = quads.tile([P, BLOCKS, QUAD_COLS], BF16, name="zT")
+                    zT[half, i // QUAD] = quads.tile([P, QUAD, BLOCKS, CHUNK], BF16, name="zT")
                 bank = turn_ps.tile([P, ROW_TILES, P], BF16, name="turned")
                 for j in range(ROW_TILES):
                     nc.tensor.transpose(bank[:, j, :], rows[half, i][:, j, c * P : (c + 1) * P], ident[:])
@@ -150,32 +148,22 @@ def tile_binarymlp_pa_t_kernel(tc, z0, g0, beta0, Wb1, bb1, out):
                 else:
                     nc.scalar.copy(out=turned_cols(half, i, c), in_=flat)
 
-            def add_rows(half, i, c):
-                if c == 0:
-                    sum_bank[half, i] = small_ps.tile([P, BLOCKS, SUM_COLS], FP32, tag="small", name="sum_bank")
+            def add_rows(i, c, sum_out, first, last):
                 for j in range(ROW_TILES):
                     nc.tensor.matmul(
-                        out=sum_bank[half, i][:, c, :],
-                        lhsT=rows[half, i][:, j, c * P : (c + 1) * P],
-                        rhs=ones[:, 0:SUM_COLS],
-                        start=(j == 0),
-                        stop=(j == ROW_TILES - 1),
+                        out=sum_out,
+                        lhsT=rows[i][:, j, c * P : (c + 1) * P],
+                        rhs=ones[:, 0 : sum_out.shape[1]],
+                        start=first and j == 0,
+                        stop=last and j == ROW_TILES - 1,
                     )
 
-            def multiply_rows(quad, k, c, gram_bank, gram_sums):
+            def gram_rows(i, c, gram_out, first, last):
                 for j in range(ROW_TILES):
-                    x = rows[1, QUAD * quad + k][:, j, c * P : (c + 1) * P]
-                    first, last = k == 0 and j == 0, k == QUAD - 1 and j == ROW_TILES - 1
-                    nc.tensor.matmul(out=gram_bank[:, c, :], lhsT=x, rhs=x, start=first, stop=last)
-                    nc.tensor.matmul(out=gram_sums[:, c, :], lhsT=x, rhs=ones[:, 0:SUM_COLS], start=first, stop=last)
-
-            def keep_sums(half, i, column, c):
-                if i == 0:
-                    nc.vector.tensor_scalar_mul(
-                        out=neg_pivot[:, half, c : c + 1], in0=sum_bank[half, i][:, c, 0:1], scalar1=-1.0 / CHUNK
+                    x = rows[i][:, j, c * P : (c + 1) * P]
+                    nc.tensor.matmul(
+                        out=gram_out, lhsT=x, rhs=x, start=first and j == 0, stop=last and j == ROW_TILES - 1
                     )
-                if c == BLOCKS - 1:
-                    nc.vector.tensor_copy(out=sums[:, half, :, column], in_=sum_bank[half, i][:, :, 0])
 
             def square(half, i, column, c):
                 unread = waste.tile([P, CHUNK], BF16)
@@ -202,14 +190,19 @@ def tile_binarymlp_pa_t_kernel(tc, z0, g0, beta0, Wb1, bb1, out):
 
             before = None
             for pair in range(pairs):
+                sum_bank = small_ps.tile([P, BLOCKS, SUM_COLS_0], FP32, tag="small", name="sum_bank")
                 for c in range(BLOCKS):
                     turn(0, 2 * pair, c, True)
-                    add_rows(0, 2 * pair, c)
+                    add_rows((0, 2 * pair), c, sum_bank[:, c, :], True, True)
                     turn(0, 2 * pair + 1, c, False)
-                    keep_sums(0, 2 * pair, pair, c)
+                    if pair == 0:
+                        nc.vector.tensor_scalar_mul(
+                            out=neg_pivot[:, 0, c : c + 1], in0=sum_bank[:, c, 0:1], scalar1=-1.0 / CHUNK
+                        )
                     if before is not None:
                         measure_pair(*before)
                     before = (pair, c)
+                nc.vector.tensor_copy(out=sums[:, 0, :, pair], in_=sum_bank[:, :, 0])
                 load_chunk(LOADS_AHEAD + 2 * pair)
                 load_chunk(LOADS_AHEAD + 2 * pair + 1)
                 if pair == 4:
@@ -247,51 +240,69 @@ def tile_binarymlp_pa_t_kernel(tc, z0, g0, beta0, Wb1, bb1, out):
                     nc.vector.bn_aggr(out=mean_var[:, 0, c, :], in_=stats[:, c, :, :].rearrange("p a s -> p (a s)"))
                 nc.vector.tensor_scalar_add(out=var_eps[:, 0, :], in0=mean_var[:, 0, :, 1], scalar1=BN_EPS)
 
-            def gather_1():
-                total = setup.tile([P, BLOCKS], FP32, name="total1")
-                nc.vector.tensor_reduce(out=total[:], in_=sums[:, 1, :, 0 : COLS_1 - 1], axis=AXIS.X, op=ALU.add)
-                nc.vector.tensor_scalar_mul(out=part_mean[:], in0=total[:], scalar1=1.0 / BATCH)
-                square_total = setup.tile([P, BLOCKS], FP32, name="square_total1")
-                nc.vector.tensor_reduce(
-                    out=square_total[:], in_=squares[:, 1, :, 0 : COLS_1 - 1], axis=AXIS.X, op=ALU.add
-                )
-                nc.vector.tensor_scalar(
-                    out=part_var[:], in0=square_total[:], scalar1=1.0 / BATCH, scalar2=BN_EPS, op0=ALU.mult, op1=ALU.add
-                )
+            gram_sum = setup.tile([P, BLOCKS, QUAD], FP32)
+            gram_acc = setup.tile([P, BLOCKS, P], FP32)
+            gram_part = setup.tile([P, BLOCKS], FP32)
 
-            def about_pivot(out_, totals):
-                half_way = setup.tile([P, BLOCKS], FP32, name="half_way")
-                nc.vector.scalar_tensor_tensor(
-                    out=half_way[:], in0=neg_pivot[:, 1, :], scalar=0.5 * QUAD_COLS, in1=totals, op0=ALU.mult, op1=ALU.add
-                )
-                nc.vector.scalar_tensor_tensor(
-                    out=out_, in0=half_way[:], scalar=2.0, in1=neg_pivot[:, 1, :], op0=ALU.mult, op1=ALU.mult
-                )
-
-            def diagonal(bank, out_):
+            def diagonal(matrix, diagonal_out):
                 picked = setup.tile([P, BLOCKS, P], FP32, name="picked")
                 nc.vector.tensor_tensor(
-                    out=picked[:], in0=bank[:], in1=ident[:].unsqueeze(1).to_broadcast([P, BLOCKS, P]), op=ALU.mult
+                    out=picked[:], in0=matrix, in1=ident[:].unsqueeze(1).to_broadcast([P, BLOCKS, P]), op=ALU.mult
                 )
-                nc.vector.tensor_reduce(out=out_, in_=picked[:], axis=AXIS.X, op=ALU.add)
+                nc.vector.tensor_reduce(out=diagonal_out, in_=picked[:], axis=AXIS.X, op=ALU.add)
 
-            def variance_1(bank):
-                totals = sums[:, 1, :, COLS_1 - 1]
-                nc.vector.scalar_tensor_tensor(
-                    out=mean_var[:, 1, :, 0], in0=totals, scalar=1.0 / BATCH, in1=part_mean[:], op0=ALU.mult, op1=ALU.add
+            part_mean = setup.tile([P, BLOCKS], FP32)
+            part_half = setup.tile([P, BLOCKS], FP32)
+            part_var = setup.tile([P, BLOCKS], FP32)
+
+            def gather_1():
+                total = setup.tile([P, BLOCKS], FP32, name="total1")
+                nc.vector.tensor_reduce(
+                    out=total[:], in_=sums[:, 1, :, 0 : SQUARED * N_QUADS], axis=AXIS.X, op=ALU.add
                 )
-                moved = setup.tile([P, BLOCKS], FP32, name="moved")
-                about_pivot(moved[:], totals)
+                gram_total = setup.tile([P, BLOCKS], FP32, name="gram_total")
+                nc.vector.tensor_reduce(
+                    out=gram_total[:], in_=gram_sum[:, :, 0 : N_QUADS - 1], axis=AXIS.X, op=ALU.add
+                )
+                square_total = setup.tile([P, BLOCKS], FP32, name="square_total1")
+                nc.vector.tensor_reduce(
+                    out=square_total[:], in_=squares[:, 1, :, 0 : SQUARED * N_QUADS], axis=AXIS.X, op=ALU.add
+                )
+                both = setup.tile([P, BLOCKS], FP32, name="both")
+                nc.vector.tensor_add(out=both[:], in0=total[:], in1=gram_total[:])
+                nc.vector.scalar_tensor_tensor(
+                    out=part_half[:],
+                    in0=neg_pivot[:, 1, :],
+                    scalar=0.5 * GRAM_ROWS,
+                    in1=gram_total[:],
+                    op0=ALU.mult,
+                    op1=ALU.add,
+                )
+                all_squares = setup.tile([P, BLOCKS], FP32, name="all_squares")
+                nc.vector.tensor_add(out=all_squares[:], in0=square_total[:], in1=gram_part[:])
+                nc.vector.tensor_scalar_mul(out=part_mean[:], in0=both[:], scalar1=1.0 / BATCH)
+                nc.vector.tensor_scalar(
+                    out=part_var[:], in0=all_squares[:], scalar1=1.0 / BATCH, scalar2=BN_EPS, op0=ALU.mult, op1=ALU.add
+                )
+
+            def variance_1(gram_bank, last_sum):
+                nc.vector.scalar_tensor_tensor(
+                    out=mean_var[:, 1, :, 0], in0=last_sum, scalar=1.0 / BATCH, in1=part_mean[:], op0=ALU.mult, op1=ALU.add
+                )
+                half_way = setup.tile([P, BLOCKS], FP32, name="half_way")
+                nc.vector.tensor_add(out=half_way[:], in0=last_sum, in1=part_half[:])
                 off = setup.tile([P, BLOCKS], FP32, name="off1")
                 nc.vector.tensor_add(out=off[:], in0=mean_var[:, 1, :, 0], in1=neg_pivot[:, 1, :])
-                so_far = setup.tile([P, BLOCKS], FP32, name="so_far")
+                moved = setup.tile([P, BLOCKS], FP32, name="moved")
                 nc.vector.scalar_tensor_tensor(
-                    out=so_far[:], in0=moved[:], scalar=1.0 / BATCH, in1=part_var[:], op0=ALU.mult, op1=ALU.add
+                    out=moved[:], in0=half_way[:], scalar=2.0 / BATCH, in1=neg_pivot[:, 1, :], op0=ALU.mult, op1=ALU.mult
                 )
                 off_sq = setup.tile([P, BLOCKS], FP32, name="off_sq1")
                 nc.vector.tensor_mul(out=off_sq[:], in0=off[:], in1=off[:])
+                so_far = setup.tile([P, BLOCKS], FP32, name="so_far")
+                nc.vector.tensor_add(out=so_far[:], in0=moved[:], in1=part_var[:])
                 raw = setup.tile([P, BLOCKS], FP32, name="raw")
-                diagonal(bank, raw[:])
+                diagonal(gram_bank, raw[:])
                 rest = setup.tile([P, BLOCKS], FP32, name="rest")
                 nc.vector.tensor_sub(out=rest[:], in0=so_far[:], in1=off_sq[:])
                 nc.vector.scalar_tensor_tensor(
@@ -324,56 +335,70 @@ def tile_binarymlp_pa_t_kernel(tc, z0, g0, beta0, Wb1, bb1, out):
 
             def normalise_0(piece):
                 if 0 <= piece < N_QUADS * BLOCKS:
-                    normalise(0, piece // BLOCKS, piece % BLOCKS, 0, QUAD_COLS, nc.vector)
+                    normalise(0, piece // BLOCKS, piece % BLOCKS, 0, QUAD, nc.vector)
 
             waiting = []
-            columns = 0
             for i in range(N_CHUNKS):
-                done = i - LAG
                 quad, part = i // QUAD, i % QUAD
-                gram = quad % 2 == 1
-                if gram and part == 0:
+                done = i - LAG
+                if part == 0:
                     gram_bank = gram_ps.tile([P, BLOCKS, P], FP32, name="gram_bank")
-                    gram_sums = small_ps.tile([P, BLOCKS, SUM_COLS], FP32, tag="small", name="gram_sums")
-                for k in range(BLOCKS):
-                    if gram:
-                        turn(1, QUAD * quad + k, part, i <= START)
-                        multiply_rows(quad, k, part, gram_bank, gram_sums)
-                    else:
-                        turn(1, i, k, i <= START)
-                        add_rows(1, i, k)
-                        keep_sums(1, i, columns, k)
-                        waiting.append((i, columns, k))
-                    if k >= 2 and i > 0:
-                        for times in range(1 if i < 12 or k == 2 else 2):
-                            if waiting:
-                                square(1, *waiting.pop(0))
-                    if done >= 0 and k == 0:
-                        regroup(0, done, True)
-                    if done >= 0 and k == 2:
-                        quantise_0(done)
-                    if i > START and k == 1:
-                        normalise_0(BLOCKS + i - START - 1)
-                if not gram:
-                    columns += 1
-                elif part == BLOCKS - 1:
-                    nc.vector.tensor_copy(out=sums[:, 1, :, columns], in_=gram_sums[:, :, 0])
-                    if columns < COLS_1 - 1:
-                        raw_1 = setup.tile([P, BLOCKS], FP32, name="raw_1")
-                        diagonal(gram_bank, raw_1[:])
-                        moved_1 = setup.tile([P, BLOCKS], FP32, name="moved_1")
-                        about_pivot(moved_1[:], sums[:, 1, :, columns])
-                        nc.vector.tensor_add(out=squares[:, 1, :, columns], in0=raw_1[:], in1=moved_1[:])
-                    columns += 1
-                if gram and part == BLOCKS - 1:
-                    first = QUAD * quad
-                elif gram:
-                    first = i + 1
-                else:
-                    first = i
-                for j in range(first, i + 1):
-                    if LOADS_AHEAD + N_CHUNKS + j < 2 * N_CHUNKS:
-                        load_chunk(LOADS_AHEAD + N_CHUNKS + j)
+                    sum_bank = small_ps.tile([P, SQUARED + 1, BLOCKS, SUM_COLS_1], FP32, tag="small", name="sum_bank_1")
+                which = part // 2
+                squared = QUAD * quad + which
+
+                def squared_unit(k):
+                    c = 2 * (part % 2) + k
+                    turn(1, squared, c, i <= START)
+                    add_rows((1, squared), c, sum_bank[:, which, c, :], True, True)
+                    waiting.append((squared, SQUARED * quad + which, c))
+
+                def gram_unit(k):
+                    gram_chunk = QUAD * quad + SQUARED + k
+                    turn(1, gram_chunk, part, i <= START)
+                    first, last = k == 0, k == QUAD - SQUARED - 1
+                    gram_rows((1, gram_chunk), part, gram_bank[:, part, :], first, last)
+                    add_rows((1, gram_chunk), part, sum_bank[:, SQUARED, part, :], first, last)
+
+                def square_next(count):
+                    for times in range(min(count, len(waiting))):
+                        square(1, *waiting.pop(0))
+
+                squared_unit(0)
+                if done >= 0:
+                    regroup(0, done, True)
+                gram_unit(0)
+                if i >= START:
+                    square_next(1)
+                if i > START:
+                    normalise_0(BLOCKS + i - START - 1)
+                gram_unit(1)
+                if done >= 0:
+                    quantise_0(done)
+                squared_unit(1)
+                if i >= START:
+                    square_next(1 if i > QUAD + START else 2)
+                if i == 1:
+                    nc.vector.tensor_scalar_mul(
+                        out=neg_pivot[:, 1, :], in0=sum_bank[:, 0, :, 0], scalar1=-1.0 / CHUNK
+                    )
+                if part == QUAD - 1:
+                    nc.vector.tensor_copy(
+                        out=sums[:, 1, :, SQUARED * quad : SQUARED * (quad + 1)],
+                        in_=sum_bank[:, 0:SQUARED, :, 0].rearrange("p s c -> p c s"),
+                    )
+                    if quad < N_QUADS - 1:
+                        nc.vector.tensor_copy(out=gram_sum[:, :, quad], in_=sum_bank[:, SQUARED, :, 0])
+                    if quad == 0:
+                        nc.scalar.copy(out=gram_acc[:], in_=gram_bank[:])
+                    elif quad < N_QUADS - 1:
+                        nc.vector.tensor_tensor(out=gram_acc[:], in0=gram_bank[:], in1=gram_acc[:], op=ALU.add)
+                    if quad == N_QUADS - 2:
+                        diagonal(gram_acc[:], gram_part[:])
+                if part == 1 or part == QUAD - 1:
+                    for j in [squared] if part == 1 else range(squared, squared + QUAD - 1):
+                        if LOADS_AHEAD + N_CHUNKS + j < 2 * N_CHUNKS:
+                            load_chunk(LOADS_AHEAD + N_CHUNKS + j)
                 if i == 0:
                     variance_0()
                 if i == 1:
@@ -391,22 +416,24 @@ def tile_binarymlp_pa_t_kernel(tc, z0, g0, beta0, Wb1, bb1, out):
                         scales=w_scales[:].rearrange("p g n -> p (g n)"),
                         in_=w_grouped[:].rearrange("p g n t -> p (g n t)"),
                     )
-                if i == N_CHUNKS - 1:
-                    gather_1()
+            for unit in waiting:
+                square(1, *unit)
+            gather_1()
 
-            variance_1(gram_bank)
+            variance_1(gram_bank[:], sum_bank[:, SQUARED, :, 0])
+            for i in range(N_CHUNKS - LAG, N_CHUNKS - 1):
+                regroup(0, i, False)
             nc.scalar.sqrt(out=std[:, 1, :], in_=var_eps[:, 1, :])
             gain_and_shift(1)
-            for i in range(N_CHUNKS - LAG, N_CHUNKS):
-                regroup(0, i, False)
+            regroup(0, N_CHUNKS - 1, False)
 
         with tc.tile_pool(name="mx", bufs=3, reuse_waits="tile") as mx, tc.tile_pool(
             name="res", bufs=3, reuse_waits="tile"
         ) as res, tc.psum_pool(name="acc_ps", bufs=8, reuse_waits="tile") as acc_ps:
 
-            pieces = [(0, c, 0, CHUNK) for c in range(BLOCKS)]
-            pieces += [(0, c, CHUNK, QUAD_COLS - CHUNK) for c in range(BLOCKS)]
-            pieces += [(quad, c, 0, QUAD_COLS) for quad in range(1, N_QUADS) for c in range(BLOCKS)]
+            pieces = [(0, c, 0, 1) for c in range(BLOCKS)]
+            pieces += [(0, c, 1, QUAD - 1) for c in range(BLOCKS)]
+            pieces += [(quad, c, 0, QUAD) for quad in range(1, N_QUADS) for c in range(BLOCKS)]
             ahead = 2 * BLOCKS + 2
 
             def normalise_1(first, count):
@@ -452,14 +479,17 @@ def tile_binarymlp_pa_t_kernel(tc, z0, g0, beta0, Wb1, bb1, out):
                     nc.sync.dma_start(out=out_rows, in_=result[:])
 
             normalise_1(0, BLOCKS)
-            for i in range(N_CHUNKS - LAG, N_CHUNKS):
-                quantise_0(i)
-            normalise_1(BLOCKS, ahead - BLOCKS)
-            accs = {}
             regroup(1, 0, False)
+            quantise_0(N_CHUNKS - 3)
+            normalise_1(BLOCKS, BLOCKS)
+            regroup(1, 1, False)
+            quantise_0(N_CHUNKS - 2)
+            normalise_1(2 * BLOCKS, ahead - 2 * BLOCKS)
+            quantise_0(N_CHUNKS - 1)
+            accs = {}
             for i in range(N_CHUNKS):
-                if i + 1 < N_CHUNKS:
-                    regroup(1, i + 1, False)
+                if i + 2 < N_CHUNKS:
+                    regroup(1, i + 2, False)
                 quantise_1(i)
                 accs[i] = multiply(i)
                 normalise_1(ahead + i, 1)

@@ -29,8 +29,8 @@ SUM_COLS_0 = 64
 SUM_COLS_1 = 4
 LOADS_AHEAD = 8
 LAG = 3
-SQUARED = 2
-GRAM_ROWS = (QUAD - SQUARED) * CHUNK * N_QUADS
+GRAM_ROWS = BATCH // 2
+LATE_STEP = 4
 START = 2
 
 
@@ -95,7 +95,12 @@ def tile_binarymlp_pa_t_kernel(tc, z0, g0, beta0, Wb1, bb1, out):
                 half, i = n // N_CHUNKS, n % N_CHUNKS
                 rows[half, i] = load.tile([P, ROW_TILES, HALF], BF16, name="rows")
                 src = z0[i * CHUNK : (i + 1) * CHUNK, half * HALF : (half + 1) * HALF]
-                nc.sync.dma_start(out=rows[half, i][:], in_=src.rearrange("(p j) f -> p j f", j=ROW_TILES))
+                src = src.rearrange("(p j) f -> p j f", j=ROW_TILES)
+                if n == 0:
+                    for j in range(ROW_TILES):
+                        nc.sync.dma_start(out=rows[half, i][:, j, :], in_=src[:, j, :])
+                else:
+                    nc.sync.dma_start(out=rows[half, i][:], in_=src)
 
             for n in range(LOADS_AHEAD):
                 load_chunk(n)
@@ -137,16 +142,28 @@ def tile_binarymlp_pa_t_kernel(tc, z0, g0, beta0, Wb1, bb1, out):
             part_var = setup.tile([P, BLOCKS], FP32)
 
             def turn(half, i, c, on_vector):
-                if (half, i // QUAD) not in zT:
-                    zT[half, i // QUAD] = quads.tile([P, QUAD, BLOCKS, CHUNK], BF16, name="zT")
-                bank = turn_ps.tile([P, ROW_TILES, P], BF16, name="turned")
-                for j in range(ROW_TILES):
-                    nc.tensor.transpose(bank[:, j, :], rows[half, i][:, j, c * P : (c + 1) * P], ident[:])
-                flat = bank[:].rearrange("p j r -> p (j r)")
-                if on_vector:
-                    nc.vector.tensor_copy(out=turned_cols(half, i, c), in_=flat)
+                quad = i[0] // QUAD
+                if (half, quad) not in zT:
+                    zT[half, quad] = quads.tile([P, QUAD, BLOCKS, CHUNK], BF16, name="zT")
+                bank = turn_ps.tile([P, 2, ROW_TILES, P], BF16, name="turned")
+                slot = 0
+                for chunk in i:
+                    for block in c:
+                        for j in range(ROW_TILES):
+                            nc.tensor.transpose(
+                                bank[:, slot, j, :], rows[half, chunk][:, j, block * P : (block + 1) * P], ident[:]
+                            )
+                        slot += 1
+                first = i[0] % QUAD
+                if len(i) == 2:
+                    dst = zT[half, quad][:, first : first + 2, c[0], :]
                 else:
-                    nc.scalar.copy(out=turned_cols(half, i, c), in_=flat)
+                    dst = zT[half, quad][:, first, c[0] : c[0] + 2, :]
+                src = bank[:].rearrange("p s j r -> p s (j r)")
+                if on_vector:
+                    nc.vector.tensor_copy(out=dst, in_=src)
+                else:
+                    nc.scalar.copy(out=dst, in_=src)
 
             def add_rows(i, c, sum_out, first, last):
                 for j in range(ROW_TILES):
@@ -166,10 +183,11 @@ def tile_binarymlp_pa_t_kernel(tc, z0, g0, beta0, Wb1, bb1, out):
                     )
 
             def square(half, i, column, c):
-                unread = waste.tile([P, CHUNK], BF16)
+                unread = waste.tile([P, 2, CHUNK], BF16)
+                first = i[0] % QUAD
                 nc.scalar.activation(
-                    out=unread[:],
-                    in_=turned_cols(half, i, c),
+                    out=unread[:, 0 : len(i), :],
+                    in_=zT[half, i[0] // QUAD][:, first : first + len(i), c, :],
                     func=ACT.Square,
                     bias=neg_pivot[:, half, c : c + 1],
                     scale=1.0,
@@ -182,36 +200,39 @@ def tile_binarymlp_pa_t_kernel(tc, z0, g0, beta0, Wb1, bb1, out):
             nc.vector.memset(stats[:, :, triples - 1, 0:1], float(pairs * CHUNK))
 
             def measure_pair(pair, c):
-                square(0, 2 * pair, pair, c)
+                square(0, [2 * pair], pair, c)
                 nc.vector.bn_stats(
                     out=stats[:, c, 2 * pair : 2 * pair + 2, :].rearrange("p a s -> p (a s)"),
                     in_=turned_cols(0, 2 * pair + 1, c),
                 )
 
-            before = None
+            before = []
             for pair in range(pairs):
                 sum_bank = small_ps.tile([P, BLOCKS, SUM_COLS_0], FP32, tag="small", name="sum_bank")
-                for c in range(BLOCKS):
-                    turn(0, 2 * pair, c, True)
-                    add_rows((0, 2 * pair), c, sum_bank[:, c, :], True, True)
-                    turn(0, 2 * pair + 1, c, False)
+                for blocks in ([0, 1], [2, 3]):
+                    turn(0, [2 * pair], blocks, True)
+                    for c in blocks:
+                        add_rows((0, 2 * pair), c, sum_bank[:, c, :], True, True)
+                    turn(0, [2 * pair + 1], blocks, False)
                     if pair == 0:
                         nc.vector.tensor_scalar_mul(
-                            out=neg_pivot[:, 0, c : c + 1], in0=sum_bank[:, c, 0:1], scalar1=-1.0 / CHUNK
+                            out=neg_pivot[:, 0, blocks[0] : blocks[0] + 2],
+                            in0=sum_bank[:, blocks[0] : blocks[0] + 2, 0],
+                            scalar1=-1.0 / CHUNK,
                         )
-                    if before is not None:
-                        measure_pair(*before)
-                    before = (pair, c)
+                    for c in before:
+                        measure_pair(*c)
+                    before = [(pair, c) for c in blocks]
                 nc.vector.tensor_copy(out=sums[:, 0, :, pair], in_=sum_bank[:, :, 0])
                 load_chunk(LOADS_AHEAD + 2 * pair)
                 load_chunk(LOADS_AHEAD + 2 * pair + 1)
                 if pair == 4:
-                    w_two = setup.tile([P, OUT_TILES, FEATS], BF16)
                     nc.vector.tensor_scalar(
-                        out=w_two[:], in0=w_rows[:], scalar1=0.0, scalar2=2.0, op0=ALU.is_ge, op1=ALU.mult
+                        out=w_rows[:], in0=w_rows[:], scalar1=0.0, scalar2=2.0, op0=ALU.is_ge, op1=ALU.mult
                     )
                     spread_vectors()
-            measure_pair(*before)
+            for c in before:
+                measure_pair(*c)
 
             mean_var = setup.tile([P, PASSES, BLOCKS, 2], FP32)
             var_eps = setup.tile([P, PASSES, BLOCKS], FP32)
@@ -258,7 +279,7 @@ def tile_binarymlp_pa_t_kernel(tc, z0, g0, beta0, Wb1, bb1, out):
             def gather_1():
                 total = setup.tile([P, BLOCKS], FP32, name="total1")
                 nc.vector.tensor_reduce(
-                    out=total[:], in_=sums[:, 1, :, 0 : SQUARED * N_QUADS], axis=AXIS.X, op=ALU.add
+                    out=total[:], in_=sums[:, 1, :, 0:N_QUADS], axis=AXIS.X, op=ALU.add
                 )
                 gram_total = setup.tile([P, BLOCKS], FP32, name="gram_total")
                 nc.vector.tensor_reduce(
@@ -266,7 +287,7 @@ def tile_binarymlp_pa_t_kernel(tc, z0, g0, beta0, Wb1, bb1, out):
                 )
                 square_total = setup.tile([P, BLOCKS], FP32, name="square_total1")
                 nc.vector.tensor_reduce(
-                    out=square_total[:], in_=squares[:, 1, :, 0 : SQUARED * N_QUADS], axis=AXIS.X, op=ALU.add
+                    out=square_total[:], in_=squares[:, 1, :, 0:N_QUADS], axis=AXIS.X, op=ALU.add
                 )
                 both = setup.tile([P, BLOCKS], FP32, name="both")
                 nc.vector.tensor_add(out=both[:], in0=total[:], in1=gram_total[:])
@@ -324,7 +345,7 @@ def tile_binarymlp_pa_t_kernel(tc, z0, g0, beta0, Wb1, bb1, out):
                 bank = turn_ps.tile([P, PACK, P], BF16, name="turned")
                 for t in range(PACK):
                     first = h * HALF + t * P
-                    nc.tensor.transpose(bank[:, t, :], w_two[:, a, first : first + P], ident[:])
+                    nc.tensor.transpose(bank[:, t, :], w_rows[:, a, first : first + P], ident[:])
                 nc.scalar.activation(
                     out=w_grouped[:, h, a * P : (a + 1) * P, :],
                     in_=bank[:].rearrange("p t n -> p n t"),
@@ -337,66 +358,49 @@ def tile_binarymlp_pa_t_kernel(tc, z0, g0, beta0, Wb1, bb1, out):
                 if 0 <= piece < N_QUADS * BLOCKS:
                     normalise(0, piece // BLOCKS, piece % BLOCKS, 0, QUAD, nc.vector)
 
-            waiting = []
+            to_square = None
             for i in range(N_CHUNKS):
-                quad, part = i // QUAD, i % QUAD
+                quad, block = i // QUAD, i % QUAD
+                squared = [QUAD * quad, QUAD * quad + 1]
+                multiplied = [QUAD * quad + 2, QUAD * quad + 3]
                 done = i - LAG
-                if part == 0:
+                if block == 0:
                     gram_bank = gram_ps.tile([P, BLOCKS, P], FP32, name="gram_bank")
-                    sum_bank = small_ps.tile([P, SQUARED + 1, BLOCKS, SUM_COLS_1], FP32, tag="small", name="sum_bank_1")
-                which = part // 2
-                squared = QUAD * quad + which
-
-                def squared_unit(k):
-                    c = 2 * (part % 2) + k
-                    turn(1, squared, c, i <= START)
-                    add_rows((1, squared), c, sum_bank[:, which, c, :], True, True)
-                    waiting.append((squared, SQUARED * quad + which, c))
-
-                def gram_unit(k):
-                    gram_chunk = QUAD * quad + SQUARED + k
-                    turn(1, gram_chunk, part, i <= START)
-                    first, last = k == 0, k == QUAD - SQUARED - 1
-                    gram_rows((1, gram_chunk), part, gram_bank[:, part, :], first, last)
-                    add_rows((1, gram_chunk), part, sum_bank[:, SQUARED, part, :], first, last)
-
-                def square_next(count):
-                    for times in range(min(count, len(waiting))):
-                        square(1, *waiting.pop(0))
-
-                squared_unit(0)
+                    sum_bank = small_ps.tile([P, 2, BLOCKS, SUM_COLS_1], FP32, tag="small", name="sum_bank_1")
+                turn(1, squared, [block], i <= START)
+                for chunk in squared:
+                    add_rows((1, chunk), block, sum_bank[:, 0, block, :], chunk == squared[0], chunk == squared[-1])
                 if done >= 0:
                     regroup(0, done, True)
-                gram_unit(0)
-                if i >= START:
-                    square_next(1)
+                if to_square is not None:
+                    square(1, *to_square)
+                to_square = (squared, quad, block)
+                turn(1, multiplied, [block], i <= START)
+                for chunk in multiplied:
+                    first, last = chunk == multiplied[0], chunk == multiplied[-1]
+                    gram_rows((1, chunk), block, gram_bank[:, block, :], first, last)
+                    add_rows((1, chunk), block, sum_bank[:, 1, block, :], first, last)
                 if i > START:
                     normalise_0(BLOCKS + i - START - 1)
-                gram_unit(1)
+                if quad == 0:
+                    nc.vector.tensor_scalar_mul(
+                        out=neg_pivot[:, 1, block : block + 1],
+                        in0=sum_bank[:, 0, block, 0:1],
+                        scalar1=-1.0 / (2 * CHUNK),
+                    )
                 if done >= 0:
                     quantise_0(done)
-                squared_unit(1)
-                if i >= START:
-                    square_next(1 if i > QUAD + START else 2)
-                if i == 1:
-                    nc.vector.tensor_scalar_mul(
-                        out=neg_pivot[:, 1, :], in0=sum_bank[:, 0, :, 0], scalar1=-1.0 / CHUNK
-                    )
-                if part == QUAD - 1:
-                    nc.vector.tensor_copy(
-                        out=sums[:, 1, :, SQUARED * quad : SQUARED * (quad + 1)],
-                        in_=sum_bank[:, 0:SQUARED, :, 0].rearrange("p s c -> p c s"),
-                    )
+                if block == BLOCKS - 1:
+                    nc.vector.tensor_copy(out=sums[:, 1, :, quad], in_=sum_bank[:, 0, :, 0])
                     if quad < N_QUADS - 1:
-                        nc.vector.tensor_copy(out=gram_sum[:, :, quad], in_=sum_bank[:, SQUARED, :, 0])
+                        nc.vector.tensor_copy(out=gram_sum[:, :, quad], in_=sum_bank[:, 1, :, 0])
                     if quad == 0:
                         nc.scalar.copy(out=gram_acc[:], in_=gram_bank[:])
                     elif quad < N_QUADS - 1:
                         nc.vector.tensor_tensor(out=gram_acc[:], in0=gram_bank[:], in1=gram_acc[:], op=ALU.add)
                     if quad == N_QUADS - 2:
                         diagonal(gram_acc[:], gram_part[:])
-                if part == 1 or part == QUAD - 1:
-                    for j in [squared] if part == 1 else range(squared, squared + QUAD - 1):
+                    for j in range(squared[0], squared[0] + QUAD):
                         if LOADS_AHEAD + N_CHUNKS + j < 2 * N_CHUNKS:
                             load_chunk(LOADS_AHEAD + N_CHUNKS + j)
                 if i == 0:
@@ -416,16 +420,14 @@ def tile_binarymlp_pa_t_kernel(tc, z0, g0, beta0, Wb1, bb1, out):
                         scales=w_scales[:].rearrange("p g n -> p (g n)"),
                         in_=w_grouped[:].rearrange("p g n t -> p (g n t)"),
                     )
-            for unit in waiting:
-                square(1, *unit)
+            square(1, *to_square)
             gather_1()
 
-            variance_1(gram_bank[:], sum_bank[:, SQUARED, :, 0])
-            for i in range(N_CHUNKS - LAG, N_CHUNKS - 1):
-                regroup(0, i, False)
+            variance_1(gram_bank[:], sum_bank[:, 1, :, 0])
+            regroup(0, N_CHUNKS - 3, False)
             nc.scalar.sqrt(out=std[:, 1, :], in_=var_eps[:, 1, :])
             gain_and_shift(1)
-            regroup(0, N_CHUNKS - 1, False)
+            regroup(0, N_CHUNKS - 2, False)
 
         with tc.tile_pool(name="mx", bufs=3, reuse_waits="tile") as mx, tc.tile_pool(
             name="res", bufs=3, reuse_waits="tile"
@@ -438,7 +440,16 @@ def tile_binarymlp_pa_t_kernel(tc, z0, g0, beta0, Wb1, bb1, out):
 
             def normalise_1(first, count):
                 for quad, c, col, width in pieces[first : first + count]:
-                    normalise(1, quad, c, col, width, nc.vector)
+                    if quad > 0 and c == BLOCKS - 1:
+                        nc.scalar.activation(
+                            out=zT[1, quad][:, :, c, :],
+                            in_=zT[1, quad][:, :, c, :],
+                            func=ACT.Identity,
+                            bias=shift[:, 1, c : c + 1],
+                            scale=gain[:, 1, c : c + 1],
+                        )
+                    else:
+                        normalise(1, quad, c, col, width, nc.vector)
 
             def quantise_1(i):
                 h_codes_1[i] = mx.tile([P, CHUNK], U32, align_bytes=64, name="h_codes_1")
@@ -479,17 +490,20 @@ def tile_binarymlp_pa_t_kernel(tc, z0, g0, beta0, Wb1, bb1, out):
                     nc.sync.dma_start(out=out_rows, in_=result[:])
 
             normalise_1(0, BLOCKS)
-            regroup(1, 0, False)
+            regroup(1, 0, True)
             quantise_0(N_CHUNKS - 3)
             normalise_1(BLOCKS, BLOCKS)
             regroup(1, 1, False)
             quantise_0(N_CHUNKS - 2)
             normalise_1(2 * BLOCKS, ahead - 2 * BLOCKS)
-            quantise_0(N_CHUNKS - 1)
             accs = {}
             for i in range(N_CHUNKS):
                 if i + 2 < N_CHUNKS:
                     regroup(1, i + 2, False)
+                if i == LATE_STEP:
+                    regroup(0, N_CHUNKS - 1, False)
+                if i == LATE_STEP + 1:
+                    quantise_0(N_CHUNKS - 1)
                 quantise_1(i)
                 accs[i] = multiply(i)
                 normalise_1(ahead + i, 1)

@@ -110,11 +110,11 @@ def tile_binarymlp_pa_t_kernel(tc, z0, g0, beta0, Wb1, bb1, out):
             vec_rows = setup.tile([P, P], BF16)
             nc.vector.memset(vec_rows[:], 0.0)
             n_vec = FEATS // P
-            nc.scalar.dma_start(out=vec_rows[0:n_vec, :], in_=g0.rearrange("(c p) -> c p", p=P))
-            nc.scalar.dma_start(out=vec_rows[n_vec : 2 * n_vec, :], in_=beta0.rearrange("(c p) -> c p", p=P))
+            nc.sync.dma_start(out=vec_rows[0:n_vec, :], in_=g0.rearrange("(c p) -> c p", p=P))
+            nc.sync.dma_start(out=vec_rows[n_vec : 2 * n_vec, :], in_=beta0.rearrange("(c p) -> c p", p=P))
             bias_row = setup.tile([P, OUTS], BF16)
             nc.vector.memset(bias_row[:], 0.0)
-            nc.scalar.dma_start(out=bias_row[0:1, :], in_=bb1.rearrange("(o n) -> o n", o=1))
+            nc.sync.dma_start(out=bias_row[0:1, :], in_=bb1.rearrange("(o n) -> o n", o=1))
             ones = setup.tile([P, P], BF16)
             nc.vector.memset(ones[:], 1.0)
 

@@ -28,10 +28,10 @@ N_QUADS = N_CHUNKS // QUAD
 SUM_COLS_0 = 64
 SUM_COLS_1 = 4
 LOADS_AHEAD = 8
-LAG = 3
+LAG = 1
 GRAM_ROWS = BATCH // 2
-LATE_STEP = 4
-START = 2
+LATE_STEPS = (12,)
+SIGN_STEP = 13
 
 
 def tile_binarymlp_pa_t_kernel(tc, z0, g0, beta0, Wb1, bb1, out):
@@ -105,7 +105,6 @@ def tile_binarymlp_pa_t_kernel(tc, z0, g0, beta0, Wb1, bb1, out):
             for n in range(LOADS_AHEAD):
                 load_chunk(n)
             w_rows = setup.tile([P, OUT_TILES, FEATS], BF16)
-            nc.sync.dma_start(out=w_rows[:], in_=Wb1.rearrange("(a p) k -> p a k", p=P))
 
             vec_rows = setup.tile([P, P], BF16)
             nc.vector.memset(vec_rows[:], 0.0)
@@ -227,9 +226,6 @@ def tile_binarymlp_pa_t_kernel(tc, z0, g0, beta0, Wb1, bb1, out):
                 load_chunk(LOADS_AHEAD + 2 * pair)
                 load_chunk(LOADS_AHEAD + 2 * pair + 1)
                 if pair == 4:
-                    nc.vector.tensor_scalar(
-                        out=w_rows[:], in0=w_rows[:], scalar1=0.0, scalar2=2.0, op0=ALU.is_ge, op1=ALU.mult
-                    )
                     spread_vectors()
             for c in before:
                 measure_pair(*c)
@@ -275,6 +271,12 @@ def tile_binarymlp_pa_t_kernel(tc, z0, g0, beta0, Wb1, bb1, out):
             part_mean = setup.tile([P, BLOCKS], FP32)
             part_half = setup.tile([P, BLOCKS], FP32)
             part_var = setup.tile([P, BLOCKS], FP32)
+
+            def normalise_first():
+                for c in range(BLOCKS):
+                    normalise(1, 0, c, 0, 2, nc.vector)
+                regroup(1, 0, True)
+                regroup(1, 1, False)
 
             def gather_1():
                 total = setup.tile([P, BLOCKS], FP32, name="total1")
@@ -358,6 +360,11 @@ def tile_binarymlp_pa_t_kernel(tc, z0, g0, beta0, Wb1, bb1, out):
                 if 0 <= piece < N_QUADS * BLOCKS:
                     normalise(0, piece // BLOCKS, piece % BLOCKS, 0, QUAD, nc.vector)
 
+            variance_0()
+            nc.scalar.sqrt(out=std[:, 0, :], in_=var_eps[:, 0, :])
+            gain_and_shift(0)
+            for piece in range(BLOCKS):
+                normalise_0(piece)
             to_square = None
             for i in range(N_CHUNKS):
                 quad, block = i // QUAD, i % QUAD
@@ -367,7 +374,7 @@ def tile_binarymlp_pa_t_kernel(tc, z0, g0, beta0, Wb1, bb1, out):
                 if block == 0:
                     gram_bank = gram_ps.tile([P, BLOCKS, P], FP32, name="gram_bank")
                     sum_bank = small_ps.tile([P, 2, BLOCKS, SUM_COLS_1], FP32, tag="small", name="sum_bank_1")
-                turn(1, squared, [block], i <= START)
+                turn(1, squared, [block], False)
                 for chunk in squared:
                     add_rows((1, chunk), block, sum_bank[:, 0, block, :], chunk == squared[0], chunk == squared[-1])
                 if done >= 0:
@@ -375,13 +382,13 @@ def tile_binarymlp_pa_t_kernel(tc, z0, g0, beta0, Wb1, bb1, out):
                 if to_square is not None:
                     square(1, *to_square)
                 to_square = (squared, quad, block)
-                turn(1, multiplied, [block], i <= START)
+                turn(1, multiplied, [block], False)
                 for chunk in multiplied:
                     first, last = chunk == multiplied[0], chunk == multiplied[-1]
                     gram_rows((1, chunk), block, gram_bank[:, block, :], first, last)
                     add_rows((1, chunk), block, sum_bank[:, 1, block, :], first, last)
-                if i > START:
-                    normalise_0(BLOCKS + i - START - 1)
+                if i > 0:
+                    normalise_0(BLOCKS + i - 1)
                 if quad == 0:
                     nc.vector.tensor_scalar_mul(
                         out=neg_pivot[:, 1, block : block + 1],
@@ -403,40 +410,36 @@ def tile_binarymlp_pa_t_kernel(tc, z0, g0, beta0, Wb1, bb1, out):
                     for j in range(squared[0], squared[0] + QUAD):
                         if LOADS_AHEAD + N_CHUNKS + j < 2 * N_CHUNKS:
                             load_chunk(LOADS_AHEAD + N_CHUNKS + j)
-                if i == 0:
-                    variance_0()
-                if i == 1:
-                    nc.scalar.sqrt(out=std[:, 0, :], in_=var_eps[:, 0, :])
-                    gain_and_shift(0)
-                if i == START:
-                    for piece in range(BLOCKS):
-                        normalise_0(piece)
-                if i < PASSES * OUT_TILES // 2:
-                    turn_weights(2 * i)
-                    turn_weights(2 * i + 1)
-                if i == 5:
-                    nc.vector.quantize_mx(
-                        out=w_codes[:].rearrange("p g n -> p (g n)").bitcast(FP8X4),
-                        scales=w_scales[:].rearrange("p g n -> p (g n)"),
-                        in_=w_grouped[:].rearrange("p g n t -> p (g n t)"),
+                if i == 2 * QUAD - 1:
+                    nc.sync.dma_start(out=w_rows[:], in_=Wb1.rearrange("(a p) k -> p a k", p=P))
+                if i == SIGN_STEP:
+                    nc.vector.tensor_scalar(
+                        out=w_rows[:], in0=w_rows[:], scalar1=0.0, scalar2=2.0, op0=ALU.is_ge, op1=ALU.mult
                     )
             square(1, *to_square)
             gather_1()
 
+            for n in range(4):
+                turn_weights(n)
             variance_1(gram_bank[:], sum_bank[:, 1, :, 0])
-            regroup(0, N_CHUNKS - 3, False)
             nc.scalar.sqrt(out=std[:, 1, :], in_=var_eps[:, 1, :])
+            for n in range(4, PASSES * OUT_TILES):
+                turn_weights(n)
             gain_and_shift(1)
-            regroup(0, N_CHUNKS - 2, False)
+            normalise_first()
+            nc.vector.quantize_mx(
+                out=w_codes[:].rearrange("p g n -> p (g n)").bitcast(FP8X4),
+                scales=w_scales[:].rearrange("p g n -> p (g n)"),
+                in_=w_grouped[:].rearrange("p g n t -> p (g n t)"),
+            )
 
         with tc.tile_pool(name="mx", bufs=3, reuse_waits="tile") as mx, tc.tile_pool(
             name="res", bufs=3, reuse_waits="tile"
         ) as res, tc.psum_pool(name="acc_ps", bufs=8, reuse_waits="tile") as acc_ps:
 
-            pieces = [(0, c, 0, 1) for c in range(BLOCKS)]
-            pieces += [(0, c, 1, QUAD - 1) for c in range(BLOCKS)]
+            pieces = [(0, c, 2, QUAD - 2) for c in range(BLOCKS)]
             pieces += [(quad, c, 0, QUAD) for quad in range(1, N_QUADS) for c in range(BLOCKS)]
-            ahead = 2 * BLOCKS + 2
+            ahead = BLOCKS + 2
 
             def normalise_1(first, count):
                 for quad, c, col, width in pieces[first : first + count]:
@@ -490,20 +493,16 @@ def tile_binarymlp_pa_t_kernel(tc, z0, g0, beta0, Wb1, bb1, out):
                     nc.sync.dma_start(out=out_rows, in_=result[:])
 
             normalise_1(0, BLOCKS)
-            regroup(1, 0, True)
-            quantise_0(N_CHUNKS - 3)
-            normalise_1(BLOCKS, BLOCKS)
-            regroup(1, 1, False)
-            quantise_0(N_CHUNKS - 2)
-            normalise_1(2 * BLOCKS, ahead - 2 * BLOCKS)
+            pass
+            normalise_1(BLOCKS, ahead - BLOCKS)
             accs = {}
             for i in range(N_CHUNKS):
                 if i + 2 < N_CHUNKS:
                     regroup(1, i + 2, False)
-                if i == LATE_STEP:
-                    regroup(0, N_CHUNKS - 1, False)
-                if i == LATE_STEP + 1:
-                    quantise_0(N_CHUNKS - 1)
+                if i in LATE_STEPS:
+                    regroup(0, N_CHUNKS - len(LATE_STEPS) + LATE_STEPS.index(i), False)
+                if i - 1 in LATE_STEPS:
+                    quantise_0(N_CHUNKS - len(LATE_STEPS) + LATE_STEPS.index(i - 1))
                 quantise_1(i)
                 accs[i] = multiply(i)
                 normalise_1(ahead + i, 1)

@@ -443,16 +443,7 @@ def tile_binarymlp_pa_t_kernel(tc, z0, g0, beta0, Wb1, bb1, out):
 
             def normalise_1(first, count):
                 for quad, c, col, width in pieces[first : first + count]:
-                    if quad > 0 and c == BLOCKS - 1:
-                        nc.scalar.activation(
-                            out=zT[1, quad][:, :, c, :],
-                            in_=zT[1, quad][:, :, c, :],
-                            func=ACT.Identity,
-                            bias=shift[:, 1, c : c + 1],
-                            scale=gain[:, 1, c : c + 1],
-                        )
-                    else:
-                        normalise(1, quad, c, col, width, nc.vector)
+                    normalise(1, quad, c, col, width, nc.vector)
 
             def quantise_1(i):
                 h_codes_1[i] = mx.tile([P, CHUNK], U32, align_bytes=64, name="h_codes_1")
@@ -486,7 +477,12 @@ def tile_binarymlp_pa_t_kernel(tc, z0, g0, beta0, Wb1, bb1, out):
                 last = i == N_CHUNKS - 1
                 result = res.tile([P, ROW_TILES, OUTS], FP32)
                 for j in range(ROW_TILES):
-                    nc.vector.tensor_tensor(out=result[:, j, :], in0=accs[j][:], in1=bias_all[:], op=ALU.add)
+                    if j < ROW_TILES - 1 or last:
+                        nc.vector.tensor_tensor(out=result[:, j, :], in0=accs[j][:], in1=bias_all[:], op=ALU.add)
+                    else:
+                        product = res.tile([P, OUTS], FP32, name="product")
+                        nc.scalar.copy(out=product[:], in_=accs[j][:])
+                        nc.gpsimd.tensor_tensor(out=result[:, j, :], in0=product[:], in1=bias_all[:], op=ALU.add)
                     if last:
                         nc.sync.dma_start(out=out_rows[:, j, :], in_=result[:, j, :])
                 if not last:

import concourse.mybir as mybir
from concourse.masks import make_identity

FP32 = mybir.dt.float32
BF16 = mybir.dt.bfloat16
U32 = mybir.dt.uint32
U8 = mybir.dt.uint8
FP8X4 = mybir.dt.float8_e4m3fn_x4
ALU = mybir.AluOpType
ACT = mybir.ActivationFunctionType
AXIS = mybir.AxisListType

P = 128
PACK = 4
BATCH, FEATS, OUTS = 8192, 1024, 512
BN_EPS = 1e-5
FLOPS = 2 * BATCH * FEATS * OUTS

PASSES = 2
HALF = FEATS // PASSES
BLOCKS = HALF // P
OUT_TILES = OUTS // P
ROW_TILES = 4
CHUNK = ROW_TILES * P
N_CHUNKS = BATCH // CHUNK
QUAD = 4
N_QUADS = N_CHUNKS // QUAD
SUM_COLS_0 = 64
SUM_COLS_1 = 4
LOADS_AHEAD = 8
LAG = 1
GRAM_ROWS = BATCH // 2
LATE_STEPS = (12,)
SIGN_STEP = 13


def tile_binarymlp_pa_t_kernel(tc, z0, g0, beta0, Wb1, bb1, out):
    nc = tc.nc
    with tc.manual_schedule(), tc.tile_pool(name="keep", bufs=1) as keep, tc.tile_pool(
        name="quads", bufs=N_QUADS + 2
    ) as quads, tc.tile_pool(name="group", bufs=4) as group:
        ident = keep.tile([P, P], BF16)
        make_identity(nc, ident[:])
        w_codes = keep.tile([P, PASSES, OUTS], U32, align_bytes=64)
        w_scales = keep.tile([P, PASSES, OUTS], U8, align_bytes=64)
        h_codes_0 = keep.tile([P, N_CHUNKS, CHUNK], U32, align_bytes=64)
        h_scales_0 = keep.tile([P, N_CHUNKS, CHUNK], U8, align_bytes=64)
        bias_all = keep.tile([P, OUTS], FP32)
        gain = keep.tile([P, PASSES, BLOCKS], FP32)
        shift = keep.tile([P, PASSES, BLOCKS], FP32)
        zT = {}
        grouped = {}
        h_codes_1 = {}
        h_scales_1 = {}

        def turned_cols(half, i, c):
            return zT[half, i // QUAD][:, i % QUAD, c, :]

        def normalise(half, quad, c, first, count, engine):
            piece = zT[half, quad][:, first : first + count, c, :]
            engine.tensor_scalar(
                out=piece,
                in0=piece,
                scalar1=gain[:, half, c : c + 1],
                scalar2=shift[:, half, c : c + 1],
                op0=ALU.mult,
                op1=ALU.add,
            )

        def regroup(half, i, on_vector):
            grouped[half, i] = group.tile([P, CHUNK, PACK], BF16, align_bytes=64, name="grouped")
            dst = grouped[half, i][:].rearrange("p (q i) t -> p q t i", i=4)
            src = zT[half, i // QUAD][:, i % QUAD, :, :].rearrange("p t (q i) -> p q t i", i=4)
            if on_vector:
                nc.vector.tensor_scalar_max(out=dst, in0=src, scalar1=0.0)
            else:
                nc.scalar.activation(out=dst, in_=src, func=ACT.Relu)

        def quantise_into(half, i, codes, scales):
            nc.vector.quantize_mx(
                out=codes.bitcast(FP8X4), scales=scales, in_=grouped[half, i][:].rearrange("p w t -> p (w t)")
            )

        def quantise_0(i):
            quantise_into(0, i, h_codes_0[:, i, :], h_scales_0[:, i, :])

        with tc.tile_pool(name="load", bufs=LOADS_AHEAD) as load, tc.tile_pool(name="waste", bufs=4) as waste, tc.tile_pool(
            name="setup", bufs=1
        ) as setup, tc.psum_pool(name="turn_ps", bufs=5) as turn_ps, tc.psum_pool(name="sum_ps", bufs=2) as small_ps, tc.psum_pool(
            name="gram_ps", bufs=1
        ) as gram_ps:
            rows = {}

            def load_chunk(n):
                half, i = n // N_CHUNKS, n % N_CHUNKS
                rows[half, i] = load.tile([P, ROW_TILES, HALF], BF16, name="rows")
                src = z0[i * CHUNK : (i + 1) * CHUNK, half * HALF : (half + 1) * HALF]
                src = src.rearrange("(p j) f -> p j f", j=ROW_TILES)
                if n == 0:
                    for j in range(ROW_TILES):
                        nc.sync.dma_start(out=rows[half, i][:, j, :], in_=src[:, j, :])
                else:
                    nc.sync.dma_start(out=rows[half, i][:], in_=src)

            for n in range(LOADS_AHEAD):
                load_chunk(n)
            w_rows = setup.tile([P, OUT_TILES, FEATS], BF16)

            vec_rows = setup.tile([P, P], BF16)
            nc.vector.memset(vec_rows[:], 0.0)
            n_vec = FEATS // P
            nc.sync.dma_start(out=vec_rows[0:n_vec, :], in_=g0.rearrange("(c p) -> c p", p=P))
            nc.sync.dma_start(out=vec_rows[n_vec : 2 * n_vec, :], in_=beta0.rearrange("(c p) -> c p", p=P))
            bias_row = setup.tile([P, OUTS], BF16)
            nc.vector.memset(bias_row[:], 0.0)
            nc.sync.dma_start(out=bias_row[0:1, :], in_=bb1.rearrange("(o n) -> o n", o=1))
            ones = setup.tile([P, P], BF16)
            nc.vector.memset(ones[:], 1.0)

            one = setup.tile([P, 1], FP32)
            nc.vector.memset(one[:], 1.0)
            warm = setup.tile([P, 1], FP32)
            nc.scalar.sqrt(out=warm[:], in_=one[:])

            vec_cols = setup.tile([P, 2, PASSES, BLOCKS], FP32)

            def spread_vectors():
                vec_ps = small_ps.tile([P, P], BF16, tag="small")
                nc.tensor.transpose(vec_ps[:], vec_rows[:], ident[:])
                nc.vector.tensor_copy(
                    out=vec_cols[:].rearrange("p v h c -> p (v h c)"), in_=vec_ps[:, 0 : 2 * n_vec]
                )
                bias_ps = small_ps.tile([P, OUTS], FP32, tag="small")
                nc.tensor.matmul(out=bias_ps[:], lhsT=ones[:], rhs=bias_row[:], start=True, stop=True)
                nc.vector.tensor_copy(out=bias_all[:], in_=bias_ps[:])

            neg_pivot = setup.tile([P, PASSES, BLOCKS], FP32)
            sums = setup.tile([P, PASSES, BLOCKS, N_CHUNKS], FP32)
            squares = setup.tile([P, PASSES, BLOCKS, N_CHUNKS], FP32)
            part_mean = setup.tile([P, BLOCKS], FP32)
            part_var = setup.tile([P, BLOCKS], FP32)

            def turn(half, i, c, on_vector):
                quad = i[0] // QUAD
                if (half, quad) not in zT:
                    zT[half, quad] = quads.tile([P, QUAD, BLOCKS, CHUNK], BF16, name="zT")
                bank = turn_ps.tile([P, 2, ROW_TILES, P], BF16, name="turned")
                slot = 0
                for chunk in i:
                    for block in c:
                        for j in range(ROW_TILES):
                            nc.tensor.transpose(
                                bank[:, slot, j, :], rows[half, chunk][:, j, block * P : (block + 1) * P], ident[:]
                            )
                        slot += 1
                first = i[0] % QUAD
                if len(i) == 2:
                    dst = zT[half, quad][:, first : first + 2, c[0], :]
                else:
                    dst = zT[half, quad][:, first, c[0] : c[0] + 2, :]
                src = bank[:].rearrange("p s j r -> p s (j r)")
                if on_vector:
                    nc.vector.tensor_copy(out=dst, in_=src)
                else:
                    nc.scalar.copy(out=dst, in_=src)

            def add_rows(i, c, sum_out, first, last):
                for j in range(ROW_TILES):
                    nc.tensor.matmul(
                        out=sum_out,
                        lhsT=rows[i][:, j, c * P : (c + 1) * P],
                        rhs=ones[:, 0 : sum_out.shape[1]],
                        start=first and j == 0,
                        stop=last and j == ROW_TILES - 1,
                    )

            def gram_rows(i, c, gram_out, first, last):
                for j in range(ROW_TILES):
                    x = rows[i][:, j, c * P : (c + 1) * P]
                    nc.tensor.matmul(
                        out=gram_out, lhsT=x, rhs=x, start=first and j == 0, stop=last and j == ROW_TILES - 1
                    )

            def square(half, i, column, c):
                unread = waste.tile([P, 2, CHUNK], BF16)
                first = i[0] % QUAD
                nc.scalar.activation(
                    out=unread[:, 0 : len(i), :],
                    in_=zT[half, i[0] // QUAD][:, first : first + len(i), c, :],
                    func=ACT.Square,
                    bias=neg_pivot[:, half, c : c + 1],
                    scale=1.0,
                    accum_out=squares[:, half, c, column : column + 1],
                )

            pairs = N_CHUNKS // 2
            triples = 2 * pairs + 1
            stats = setup.tile([P, BLOCKS, triples, 3], FP32)
            nc.vector.memset(stats[:, :, triples - 1, 0:1], float(pairs * CHUNK))

            def measure_pair(pair, c):
                square(0, [2 * pair], pair, c)
                nc.vector.bn_stats(
                    out=stats[:, c, 2 * pair : 2 * pair + 2, :].rearrange("p a s -> p (a s)"),
                    in_=turned_cols(0, 2 * pair + 1, c),
                )

            before = []
            for pair in range(pairs):
                sum_bank = small_ps.tile([P, BLOCKS, SUM_COLS_0], FP32, tag="small", name="sum_bank")
                for blocks in ([0, 1], [2, 3]):
                    turn(0, [2 * pair], blocks, True)
                    for c in blocks:
                        add_rows((0, 2 * pair), c, sum_bank[:, c, :], True, True)
                    turn(0, [2 * pair + 1], blocks, False)
                    if pair == 0:
                        nc.vector.tensor_scalar_mul(
                            out=neg_pivot[:, 0, blocks[0] : blocks[0] + 2],
                            in0=sum_bank[:, blocks[0] : blocks[0] + 2, 0],
                            scalar1=-1.0 / CHUNK,
                        )
                    for c in before:
                        measure_pair(*c)
                    before = [(pair, c) for c in blocks]
                nc.vector.tensor_copy(out=sums[:, 0, :, pair], in_=sum_bank[:, :, 0])
                load_chunk(LOADS_AHEAD + 2 * pair)
                load_chunk(LOADS_AHEAD + 2 * pair + 1)
                if pair == 4:
                    spread_vectors()
            for c in before:
                measure_pair(*c)

            mean_var = setup.tile([P, PASSES, BLOCKS, 2], FP32)
            var_eps = setup.tile([P, PASSES, BLOCKS], FP32)
            std = setup.tile([P, PASSES, BLOCKS], FP32)

            def sum_up(half, columns, mean, spread):
                count = float(columns * CHUNK)
                total = setup.tile([P, BLOCKS], FP32, name=f"total{half}")
                nc.vector.tensor_reduce(out=total[:], in_=sums[:, half, :, 0:columns], axis=AXIS.X, op=ALU.add)
                square_total = setup.tile([P, BLOCKS], FP32, name=f"square_total{half}")
                nc.vector.tensor_reduce(
                    out=square_total[:], in_=squares[:, half, :, 0:columns], axis=AXIS.X, op=ALU.add
                )
                nc.vector.tensor_scalar_mul(out=mean, in0=total[:], scalar1=1.0 / count)
                off = setup.tile([P, BLOCKS], FP32, name=f"off{half}")
                nc.vector.tensor_add(out=off[:], in0=mean, in1=neg_pivot[:, half, :])
                off_sq = setup.tile([P, BLOCKS], FP32, name=f"off_sq{half}")
                nc.vector.tensor_mul(out=off_sq[:], in0=off[:], in1=off[:])
                nc.vector.scalar_tensor_tensor(
                    out=spread, in0=off_sq[:], scalar=-count, in1=square_total[:], op0=ALU.mult, op1=ALU.add
                )

            def variance_0():
                sum_up(0, pairs, stats[:, :, triples - 1, 1], stats[:, :, triples - 1, 2])
                for c in range(BLOCKS):
                    nc.vector.bn_aggr(out=mean_var[:, 0, c, :], in_=stats[:, c, :, :].rearrange("p a s -> p (a s)"))
                nc.vector.tensor_scalar_add(out=var_eps[:, 0, :], in0=mean_var[:, 0, :, 1], scalar1=BN_EPS)

            gram_sum = setup.tile([P, BLOCKS, QUAD], FP32)
            gram_acc = setup.tile([P, BLOCKS, P], FP32)
            gram_part = setup.tile([P, BLOCKS], FP32)

            def diagonal(matrix, diagonal_out):
                picked = setup.tile([P, BLOCKS, P], FP32, name="picked")
                nc.vector.tensor_tensor(
                    out=picked[:], in0=matrix, in1=ident[:].unsqueeze(1).to_broadcast([P, BLOCKS, P]), op=ALU.mult
                )
                nc.vector.tensor_reduce(out=diagonal_out, in_=picked[:], axis=AXIS.X, op=ALU.add)

            part_mean = setup.tile([P, BLOCKS], FP32)
            part_half = setup.tile([P, BLOCKS], FP32)
            part_var = setup.tile([P, BLOCKS], FP32)

            def normalise_first():
                for c in range(BLOCKS):
                    normalise(1, 0, c, 0, 2, nc.vector)
                regroup(1, 0, True)
                regroup(1, 1, False)

            def gather_1():
                total = setup.tile([P, BLOCKS], FP32, name="total1")
                nc.vector.tensor_reduce(
                    out=total[:], in_=sums[:, 1, :, 0:N_QUADS], axis=AXIS.X, op=ALU.add
                )
                gram_total = setup.tile([P, BLOCKS], FP32, name="gram_total")
                nc.vector.tensor_reduce(
                    out=gram_total[:], in_=gram_sum[:, :, 0 : N_QUADS - 1], axis=AXIS.X, op=ALU.add
                )
                square_total = setup.tile([P, BLOCKS], FP32, name="square_total1")
                nc.vector.tensor_reduce(
                    out=square_total[:], in_=squares[:, 1, :, 0:N_QUADS], axis=AXIS.X, op=ALU.add
                )
                both = setup.tile([P, BLOCKS], FP32, name="both")
                nc.vector.tensor_add(out=both[:], in0=total[:], in1=gram_total[:])
                nc.vector.scalar_tensor_tensor(
                    out=part_half[:],
                    in0=neg_pivot[:, 1, :],
                    scalar=0.5 * GRAM_ROWS,
                    in1=gram_total[:],
                    op0=ALU.mult,
                    op1=ALU.add,
                )
                all_squares = setup.tile([P, BLOCKS], FP32, name="all_squares")
                nc.vector.tensor_add(out=all_squares[:], in0=square_total[:], in1=gram_part[:])
                nc.vector.tensor_scalar_mul(out=part_mean[:], in0=both[:], scalar1=1.0 / BATCH)
                nc.vector.tensor_scalar(
                    out=part_var[:], in0=all_squares[:], scalar1=1.0 / BATCH, scalar2=BN_EPS, op0=ALU.mult, op1=ALU.add
                )

            def variance_1(gram_bank, last_sum):
                nc.vector.scalar_tensor_tensor(
                    out=mean_var[:, 1, :, 0], in0=last_sum, scalar=1.0 / BATCH, in1=part_mean[:], op0=ALU.mult, op1=ALU.add
                )
                half_way = setup.tile([P, BLOCKS], FP32, name="half_way")
                nc.vector.tensor_add(out=half_way[:], in0=last_sum, in1=part_half[:])
                off = setup.tile([P, BLOCKS], FP32, name="off1")
                nc.vector.tensor_add(out=off[:], in0=mean_var[:, 1, :, 0], in1=neg_pivot[:, 1, :])
                moved = setup.tile([P, BLOCKS], FP32, name="moved")
                nc.vector.scalar_tensor_tensor(
                    out=moved[:], in0=half_way[:], scalar=2.0 / BATCH, in1=neg_pivot[:, 1, :], op0=ALU.mult, op1=ALU.mult
                )
                off_sq = setup.tile([P, BLOCKS], FP32, name="off_sq1")
                nc.vector.tensor_mul(out=off_sq[:], in0=off[:], in1=off[:])
                so_far = setup.tile([P, BLOCKS], FP32, name="so_far")
                nc.vector.tensor_add(out=so_far[:], in0=moved[:], in1=part_var[:])
                raw = setup.tile([P, BLOCKS], FP32, name="raw")
                diagonal(gram_bank, raw[:])
                rest = setup.tile([P, BLOCKS], FP32, name="rest")
                nc.vector.tensor_sub(out=rest[:], in0=so_far[:], in1=off_sq[:])
                nc.vector.scalar_tensor_tensor(
                    out=var_eps[:, 1, :], in0=raw[:], scalar=1.0 / BATCH, in1=rest[:], op0=ALU.mult, op1=ALU.add
                )

            def gain_and_shift(half):
                rstd = setup.tile([P, BLOCKS], FP32, name=f"rstd{half}")
                nc.vector.reciprocal(out=rstd[:], in_=std[:, half, :])
                nc.vector.tensor_mul(out=gain[:, half, :], in0=vec_cols[:, 0, half, :], in1=rstd[:])
                mean_gain = setup.tile([P, BLOCKS], FP32, name=f"mean_gain{half}")
                nc.vector.tensor_mul(out=mean_gain[:], in0=mean_var[:, half, :, 0], in1=gain[:, half, :])
                nc.vector.tensor_sub(out=shift[:, half, :], in0=vec_cols[:, 1, half, :], in1=mean_gain[:])

            w_grouped = setup.tile([P, PASSES, OUTS, PACK], BF16, align_bytes=64)

            def turn_weights(n):
                h, a = n // OUT_TILES, n % OUT_TILES
                bank = turn_ps.tile([P, PACK, P], BF16, name="turned")
                for t in range(PACK):
                    first = h * HALF + t * P
                    nc.tensor.transpose(bank[:, t, :], w_rows[:, a, first : first + P], ident[:])
                nc.scalar.activation(
                    out=w_grouped[:, h, a * P : (a + 1) * P, :],
                    in_=bank[:].rearrange("p t n -> p n t"),
                    func=ACT.Copy,
                    bias=-1.0,
                    scale=1.0,
                )

            def normalise_0(piece):
                if 0 <= piece < N_QUADS * BLOCKS:
                    normalise(0, piece // BLOCKS, piece % BLOCKS, 0, QUAD, nc.vector)

            variance_0()
            nc.scalar.sqrt(out=std[:, 0, :], in_=var_eps[:, 0, :])
            gain_and_shift(0)
            for piece in range(BLOCKS):
                normalise_0(piece)
            to_square = None
            for i in range(N_CHUNKS):
                quad, block = i // QUAD, i % QUAD
                squared = [QUAD * quad, QUAD * quad + 1]
                multiplied = [QUAD * quad + 2, QUAD * quad + 3]
                done = i - LAG
                if block == 0:
                    gram_bank = gram_ps.tile([P, BLOCKS, P], FP32, name="gram_bank")
                    sum_bank = small_ps.tile([P, 2, BLOCKS, SUM_COLS_1], FP32, tag="small", name="sum_bank_1")
                turn(1, squared, [block], False)
                for chunk in squared:
                    add_rows((1, chunk), block, sum_bank[:, 0, block, :], chunk == squared[0], chunk == squared[-1])
                if done >= 0:
                    regroup(0, done, True)
                if to_square is not None:
                    square(1, *to_square)
                to_square = (squared, quad, block)
                turn(1, multiplied, [block], False)
                for chunk in multiplied:
                    first, last = chunk == multiplied[0], chunk == multiplied[-1]
                    gram_rows((1, chunk), block, gram_bank[:, block, :], first, last)
                    add_rows((1, chunk), block, sum_bank[:, 1, block, :], first, last)
                if i > 0:
                    normalise_0(BLOCKS + i - 1)
                if quad == 0:
                    nc.vector.tensor_scalar_mul(
                        out=neg_pivot[:, 1, block : block + 1],
                        in0=sum_bank[:, 0, block, 0:1],
                        scalar1=-1.0 / (2 * CHUNK),
                    )
                if done >= 0:
                    quantise_0(done)
                if block == BLOCKS - 1:
                    nc.vector.tensor_copy(out=sums[:, 1, :, quad], in_=sum_bank[:, 0, :, 0])
                    if quad < N_QUADS - 1:
                        nc.vector.tensor_copy(out=gram_sum[:, :, quad], in_=sum_bank[:, 1, :, 0])
                    if quad == 0:
                        nc.scalar.copy(out=gram_acc[:], in_=gram_bank[:])
                    elif quad < N_QUADS - 1:
                        nc.vector.tensor_tensor(out=gram_acc[:], in0=gram_bank[:], in1=gram_acc[:], op=ALU.add)
                    if quad == N_QUADS - 2:
                        diagonal(gram_acc[:], gram_part[:])
                    for j in range(squared[0], squared[0] + QUAD):
                        if LOADS_AHEAD + N_CHUNKS + j < 2 * N_CHUNKS:
                            load_chunk(LOADS_AHEAD + N_CHUNKS + j)
                if i == 2 * QUAD - 1:
                    nc.sync.dma_start(out=w_rows[:], in_=Wb1.rearrange("(a p) k -> p a k", p=P))
                if i == SIGN_STEP:
                    nc.vector.tensor_scalar(
                        out=w_rows[:], in0=w_rows[:], scalar1=0.0, scalar2=2.0, op0=ALU.is_ge, op1=ALU.mult
                    )
            square(1, *to_square)
            gather_1()

            for n in range(4):
                turn_weights(n)
            variance_1(gram_bank[:], sum_bank[:, 1, :, 0])
            nc.scalar.sqrt(out=std[:, 1, :], in_=var_eps[:, 1, :])
            for n in range(4, PASSES * OUT_TILES):
                turn_weights(n)
            gain_and_shift(1)
            normalise_first()
            nc.vector.quantize_mx(
                out=w_codes[:].rearrange("p g n -> p (g n)").bitcast(FP8X4),
                scales=w_scales[:].rearrange("p g n -> p (g n)"),
                in_=w_grouped[:].rearrange("p g n t -> p (g n t)"),
            )

        with tc.tile_pool(name="mx", bufs=3, reuse_waits="tile") as mx, tc.tile_pool(
            name="res", bufs=3, reuse_waits="tile"
        ) as res, tc.psum_pool(name="acc_ps", bufs=8, reuse_waits="tile") as acc_ps:

            pieces = [(0, c, 2, QUAD - 2) for c in range(BLOCKS)]
            pieces += [(quad, c, 0, QUAD) for quad in range(1, N_QUADS) for c in range(BLOCKS)]
            ahead = BLOCKS + 2

            def normalise_1(first, count):
                for quad, c, col, width in pieces[first : first + count]:
                    normalise(1, quad, c, col, width, nc.vector)

            def quantise_1(i):
                h_codes_1[i] = mx.tile([P, CHUNK], U32, align_bytes=64, name="h_codes_1")
                h_scales_1[i] = mx.tile([P, CHUNK], U8, align_bytes=64, name="h_scales_1")
                quantise_into(1, i, h_codes_1[i][:], h_scales_1[i][:])

            def multiply(i):
                accs = []
                for j in range(ROW_TILES):
                    cols = slice(j * P, (j + 1) * P)
                    acc = acc_ps.tile([P, OUTS], FP32)
                    halves = [
                        (h_codes_0[:, i, cols], h_scales_0[:, i, cols]),
                        (h_codes_1[i][:, cols], h_scales_1[i][:, cols]),
                    ]
                    for g in range(PASSES):
                        nc.tensor.matmul_mx(
                            out=acc[:],
                            lhsT=halves[g][0].bitcast(FP8X4),
                            lhsT_scale=halves[g][1],
                            rhs=w_codes[:, g, :].bitcast(FP8X4),
                            rhs_scale=w_scales[:, g, :],
                            start=(g == 0),
                            stop=(g == PASSES - 1),
                        )
                    accs.append(acc)
                return accs

            def finish(i, accs):
                out_rows = out[i * CHUNK : (i + 1) * CHUNK, :].rearrange("(p j) n -> p j n", j=ROW_TILES)
                last = i == N_CHUNKS - 1
                result = res.tile([P, ROW_TILES, OUTS], FP32)
                for j in range(ROW_TILES):
                    if j < ROW_TILES - 1 or last:
                        nc.vector.tensor_tensor(out=result[:, j, :], in0=accs[j][:], in1=bias_all[:], op=ALU.add)
                    else:
                        product = res.tile([P, OUTS], FP32, name="product")
                        nc.scalar.copy(out=product[:], in_=accs[j][:])
                        nc.gpsimd.tensor_tensor(out=result[:, j, :], in0=product[:], in1=bias_all[:], op=ALU.add)
                    if last:
                        nc.sync.dma_start(out=out_rows[:, j, :], in_=result[:, j, :])
                if not last:
                    nc.sync.dma_start(out=out_rows, in_=result[:])

            normalise_1(0, BLOCKS)
            pass
            normalise_1(BLOCKS, ahead - BLOCKS)
            accs = {}
            for i in range(N_CHUNKS):
                if i + 2 < N_CHUNKS:
                    regroup(1, i + 2, False)
                if i in LATE_STEPS:
                    regroup(0, N_CHUNKS - len(LATE_STEPS) + LATE_STEPS.index(i), False)
                if i - 1 in LATE_STEPS:
                    quantise_0(N_CHUNKS - len(LATE_STEPS) + LATE_STEPS.index(i - 1))
                quantise_1(i)
                accs[i] = multiply(i)
                normalise_1(ahead + i, 1)
                if i > 0:
                    finish(i - 1, accs[i - 1])
            finish(N_CHUNKS - 1, accs[N_CHUNKS - 1])
